import numpy as np
import ml_dtypes


def mxq(x, axis, fmt="e4m3"):
    dtype, down = {"e4m3": (ml_dtypes.float8_e4m3fn, 7), "e5m2": (ml_dtypes.float8_e5m2, 14)}[fmt]
    v = np.moveaxis(np.asarray(x, np.float32).astype(ml_dtypes.bfloat16).astype(np.float64), axis, -1)
    blocks = v.reshape(v.shape[:-1] + (-1, 32))
    amax = np.abs(blocks).max(-1, keepdims=True)
    byte = np.maximum(np.where(amax > 0, np.frexp(amax)[1] - 1 + 127, 0) - down, 1)
    scale = np.exp2(byte - 127.0)
    codes = (blocks / scale).astype(np.float32).astype(dtype).astype(np.float64)
    return np.moveaxis((codes * scale).reshape(v.shape), -1, axis)


WIDE = False


def mx_kscale(k):
    if not WIDE:
        return np.ones(k)
    levels = np.array([10, -10, 5, -5, 0])
    a = np.random.permutation(np.resize(levels, k // 512 * 4)).reshape(k // 512, 4)
    idx = np.arange(k)
    return np.exp2(a[idx // 512, idx % 128 // 32])


BF16 = ml_dtypes.bfloat16


def bf(x):
    return np.asarray(x, np.float32).astype(BF16)


def f64(x):
    return np.asarray(x).astype(np.float64)


B, P, K, C = 80, 24, 512, 6
EPS = 1e-5


def color_layernorm(x, gamma, beta):
    mean = np.mean(x, axis=-1, keepdims=True)
    var = np.mean(np.square(x - mean), axis=-1, keepdims=True)
    xn = (x - mean) / np.sqrt(var + EPS)
    xn = xn.reshape(*x.shape[:-1], K, C)
    xn = xn * gamma[:, None] + beta[:, None]
    return xn.reshape(x.shape)


def color_conv(x, weight, bias):
    xr = x.reshape(B, P, K, C)
    alpha = weight[:, :, 0] - weight[:, :, 1]
    beta_w = weight[:, :, 1]
    term1 = mxq(alpha, 1, "e4m3") @ mxq(xr, 2, "e4m3")
    x_sum = xr.sum(axis=3)
    term2 = mxq(x_sum, 2, "e4m3") @ mxq(beta_w, 1, "e4m3").T
    out = term1 + term2[..., None] + bias[None, None, :, None]
    return out.reshape(B, P, K * C)


def setup_inputs():
    s = mx_kscale(K)
    bound = np.sqrt(3.0 / K)
    return {"x": bf(np.random.standard_normal((B, P, C * K))),
            "conv_weight": bf(np.random.uniform(-bound, bound, (K, K, 2)) / s[None, :, None]),
            "conv_bias": bf(np.random.standard_normal(K) * 0.5),
            "norm_weight": bf((1.0 + 0.1 * np.random.standard_normal(K)) * s),
            "norm_bias": bf(0.1 * np.random.standard_normal(K) * s)}


def reference(x, conv_weight, conv_bias, norm_weight, norm_bias):
    x = f64(x)
    h = color_layernorm(x, f64(norm_weight), f64(norm_bias))
    h = color_conv(h, f64(conv_weight), f64(conv_bias))
    return x + np.maximum(h, 0.0)

@@ -1,0 +1,231 @@
+from contextlib import ExitStack
+
+import concourse.mybir as mybir
+from concourse.masks import make_identity
+
+F32 = mybir.dt.float32
+BF16 = mybir.dt.bfloat16
+U32 = mybir.dt.uint32
+U8 = mybir.dt.uint8
+FP8X4 = mybir.dt.float8_e4m3fn_x4
+ALU = mybir.AluOpType
+ACT = mybir.ActivationFunctionType
+
+P = 128
+K = 512
+C = 6
+T = 4
+ROW = K * C
+NPOS = 80 * 24
+NT = NPOS // P
+EPS = 1e-5
+HCOLS = (C + 1) * P
+
+FLOPS = 2 * NPOS * C * K * K + 2 * NPOS * K * K
+
+
+def tile_colorresblock_t_kernel(tc, x, conv_weight, conv_bias, norm_weight, norm_bias, out):
+    nc = tc.nc
+    xr = x.flatten_outer_dims()
+    outr = out.flatten_outer_dims()
+
+    with ExitStack() as ctx:
+        const = ctx.enter_context(tc.tile_pool(name="const", bufs=1))
+        xpool = ctx.enter_context(tc.tile_pool(name="xpool", bufs=6))
+        small = ctx.enter_context(tc.tile_pool(name="small", bufs=4))
+        work = ctx.enter_context(tc.tile_pool(name="work", bufs=2))
+        pst = ctx.enter_context(tc.psum_pool(name="pst", bufs=4))
+        psm = ctx.enter_context(tc.psum_pool(name="psm", bufs=4))
+
+        st = {}
+
+        def load(i):
+            xt = xpool.tile([P, ROW], BF16, name="xt")
+            nc.sync.dma_start(out=xt[:], in_=xr[i * P : (i + 1) * P, :])
+            st[("x", i)] = xt
+
+        load(0)
+
+        ident = const.tile([P, P], F32, name="ident")
+        make_identity(nc, ident[:])
+        negh = const.tile([P, 1], F32, name="negh")
+        nc.vector.memset(negh[:], -0.5)
+
+        wraw = const.tile([P, 4, 2 * K], BF16, name="wraw")
+        nc.sync.dma_start(out=wraw[:], in_=conv_weight.rearrange("(c p) k s -> p c (k s)", p=P))
+        graw = const.tile([P, T], BF16, name="graw")
+        nc.sync.dma_start(out=graw[:], in_=norm_weight.rearrange("(p t) -> p t", t=T))
+        braw = const.tile([P, T], BF16, name="braw")
+        nc.sync.dma_start(out=braw[:], in_=norm_bias.rearrange("(p t) -> p t", t=T))
+        load(1)
+        cbraw = const.tile([P, K], BF16, name="cbraw")
+        nc.sync.dma_start(out=cbraw[:], in_=conv_bias.partition_broadcast(P))
+
+        gcol = const.tile([P, T], F32, name="gcol")
+        nc.vector.tensor_copy(out=gcol[:], in_=graw[:])
+        bcol = const.tile([P, T], F32, name="bcol")
+        nc.vector.tensor_copy(out=bcol[:], in_=braw[:])
+        b6col = const.tile([P, T], F32, name="b6col")
+        nc.vector.tensor_scalar(out=b6col[:], in0=braw[:], scalar1=float(C), scalar2=None, op0=ALU.mult)
+        cb = const.tile([P, K], F32, name="cb")
+        nc.vector.tensor_copy(out=cb[:], in_=cbraw[:])
+
+        wv = wraw[:].rearrange("p c (q t s) -> p c t q s", t=T, s=2)
+        wf_a = const.tile([P, 4, T, P], F32, name="wf_a")
+        nc.vector.tensor_tensor(out=wf_a[:], in0=wv[:, :, :, :, 0], in1=wv[:, :, :, :, 1], op=ALU.subtract)
+        wf_b = const.tile([P, 4, T, P], F32, name="wf_b")
+        nc.vector.tensor_copy(out=wf_b[:], in_=wv[:, :, :, :, 1])
+
+        wcodes = []
+        wscales = []
+        for m, wf in enumerate((wf_a, wf_b)):
+            wg = const.tile([P, K, T], BF16, name="wg%d" % m, align_bytes=64)
+            for oc in range(4):
+                pw = pst.tile([P, 512], F32, name="pw", tag="pt")
+                for t in range(T):
+                    nc.tensor.transpose(pw[:, t * P : (t + 1) * P], wf[:, oc, t, :], ident[:])
+                src = pw[:].rearrange("p (t o) -> p o t", t=T)
+                dst = wg[:, oc * P : (oc + 1) * P, :]
+                if oc % 2 == 0:
+                    nc.vector.tensor_copy(out=dst, in_=src)
+                else:
+                    nc.scalar.copy(out=dst, in_=src)
+            wc = const.tile([P, K], U32, name="wc%d" % m, align_bytes=64)
+            ws = const.tile([P, K], U8, name="ws%d" % m, align_bytes=64)
+            nc.vector.quantize_mx(
+                out=wc[:].bitcast(FP8X4), scales=ws[:], in_=wg[:].rearrange("p o t -> p (o t)")
+            )
+            wcodes.append(wc)
+            wscales.append(ws)
+
+        def stats(i):
+            xt = st[("x", i)]
+            junk = work.tile([P, ROW], BF16, name="junk", bufs=1)
+            sx = small.tile([P, 1], F32, name="sx")
+            nc.scalar.activation(out=junk[:], in_=xt[:], func=ACT.Identity, accum_out=sx[:])
+            negmean = small.tile([P, 1], F32, name="negmean")
+            nc.vector.tensor_scalar(out=negmean[:], in0=sx[:], scalar1=-1.0 / ROW, scalar2=None, op0=ALU.mult)
+            junk2 = work.tile([P, ROW], BF16, name="junk2", tag="junk", bufs=1)
+            ssq = small.tile([P, 1], F32, name="ssq")
+            nc.scalar.activation(
+                out=junk2[:], in_=xt[:], func=ACT.Square, bias=negmean[:], scale=1.0, accum_out=ssq[:]
+            )
+            var = small.tile([P, 1], F32, name="var")
+            nc.vector.tensor_scalar(
+                out=var[:], in0=ssq[:], scalar1=1.0 / ROW, scalar2=EPS, op0=ALU.mult, op1=ALU.add
+            )
+            rstd = small.tile([P, 1], F32, name="rstd")
+            nc.gpsimd.tensor_tensor(out=rstd[:], in0=var[:], in1=negh[:], op=ALU.pow)
+            st[("nm", i)] = negmean
+            st[("rs", i)] = rstd
+
+        def front(i):
+            xt = st[("x", i)]
+            negmean = st[("nm", i)]
+            rstd = st[("rs", i)]
+            xv = xt[:].rearrange("p (q t d) -> p t d q", t=T, d=C)
+            u = work.tile([P, T, C, P], F32, name="u")
+            ht = work.tile([P, T, HCOLS], BF16, name="ht")
+            for t in range(T):
+                nc.gpsimd.tensor_scalar(
+                    out=u[:, t, :, :],
+                    in0=xv[:, t, :, :],
+                    scalar1=negmean[:],
+                    scalar2=rstd[:],
+                    op0=ALU.add,
+                    op1=ALU.mult,
+                )
+            for t in range(T):
+                pa = pst.tile([P, 512], F32, name="pa", tag="pt")
+                for d in range(4):
+                    nc.tensor.transpose(pa[:, d * P : (d + 1) * P], u[:, t, d, :], ident[:])
+                pb = pst.tile([P, 512], F32, name="pb", tag="pt")
+                for d in range(4, C):
+                    nc.tensor.transpose(pb[:, (d - 4) * P : (d - 3) * P], u[:, t, d, :], ident[:])
+                for d in range(C):
+                    nc.tensor.matmul(
+                        pb[:, 2 * P : 3 * P],
+                        lhsT=u[:, t, d, :],
+                        rhs=ident[:],
+                        is_transpose=True,
+                        start=(d == 0),
+                        stop=(d == C - 1),
+                    )
+                g = gcol[:, t : t + 1]
+                nc.scalar.activation(
+                    out=ht[:, t, 0 : 4 * P], in_=pa[:], func=ACT.Identity, scale=g, bias=bcol[:, t : t + 1]
+                )
+                nc.scalar.activation(
+                    out=ht[:, t, 4 * P : 6 * P], in_=pb[:, 0 : 2 * P], func=ACT.Identity, scale=g,
+                    bias=bcol[:, t : t + 1],
+                )
+                nc.scalar.activation(
+                    out=ht[:, t, 6 * P : 7 * P], in_=pb[:, 2 * P : 3 * P], func=ACT.Identity, scale=g,
+                    bias=b6col[:, t : t + 1],
+                )
+            st[("ht", i)] = ht
+
+        def back(i):
+            xt = st[("x", i)]
+            ht = st[("ht", i)]
+            gr = work.tile([P, HCOLS, T], BF16, name="gr", align_bytes=64)
+            nc.vector.tensor_copy(out=gr[:], in_=ht[:].rearrange("p t c -> p c t"))
+            hc = work.tile([P, HCOLS], U32, name="hc", align_bytes=64)
+            hsc = work.tile([P, HCOLS], U8, name="hsc", align_bytes=64)
+            for lo, hi in ((0, 512), (512, 768), (768, 896)):
+                nc.vector.quantize_mx(
+                    out=hc[:, lo:hi].bitcast(FP8X4),
+                    scales=hsc[:, lo:hi],
+                    in_=gr[:, lo:hi, :].rearrange("p c t -> p (c t)"),
+                )
+            tt = work.tile([P, 2, 3 * K], F32, name="tt")
+            for e in range(2):
+                for oc in range(4):
+                    pm = psm.tile([P, 512], F32, name="pm")
+                    ocs = slice(oc * P, (oc + 1) * P)
+                    for j in range(3):
+                        d = 2 * j + e
+                        nc.tensor.matmul_mx(
+                            out=pm[:, j * P : (j + 1) * P],
+                            lhsT=hc[:, d * P : (d + 1) * P].bitcast(FP8X4),
+                            lhsT_scale=hsc[:, d * P : (d + 1) * P],
+                            rhs=wcodes[0][:, ocs].bitcast(FP8X4),
+                            rhs_scale=wscales[0][:, ocs],
+                            start=True,
+                            stop=False,
+                        )
+                        nc.tensor.matmul_mx(
+                            out=pm[:, j * P : (j + 1) * P],
+                            lhsT=hc[:, C * P : (C + 1) * P].bitcast(FP8X4),
+                            lhsT_scale=hsc[:, C * P : (C + 1) * P],
+                            rhs=wcodes[1][:, ocs].bitcast(FP8X4),
+                            rhs_scale=wscales[1][:, ocs],
+                            start=False,
+                            stop=True,
+                        )
+                    nc.vector.tensor_tensor(
+                        out=tt[:, e, oc * 3 * P : (oc + 1) * 3 * P].rearrange("p (o j) -> p o j", j=3),
+                        in0=pm[:, 0 : 3 * P].rearrange("p (j o) -> p o j", j=3),
+                        in1=cb[:, ocs].unsqueeze(2).to_broadcast([P, P, 3]),
+                        op=ALU.add,
+                    )
+            ot = work.tile([P, ROW], F32, name="ot")
+            nc.vector.scalar_tensor_tensor(
+                out=ot[:].rearrange("p (a e) -> p a e", e=2),
+                in0=tt[:].rearrange("p e a -> p a e"),
+                scalar=0.0,
+                in1=xt[:].rearrange("p (a e) -> p a e", e=2),
+                op0=ALU.max,
+                op1=ALU.add,
+            )
+            nc.sync.dma_start(out=outr[i * P : (i + 1) * P, :], in_=ot[:])
+
+        for n in range(NT + 2):
+            if n + 2 < NT:
+                load(n + 2)
+            if n < NT:
+                stats(n)
+            if 0 <= n - 2:
+                back(n - 2)
+            if 0 <= n - 1 < NT:
+                front(n - 1)

@@ -127,7 +127,7 @@ def tile_colorresblock_t_kernel(tc, x, conv_weight, conv_bias, norm_weight, norm
             u = work.tile([P, T, C, P], F32, name="u")
             ht = work.tile([P, T, HCOLS], BF16, name="ht")
             for t in range(T):
-                nc.gpsimd.tensor_scalar(
+                nc.vector.tensor_scalar(
                     out=u[:, t, :, :],
                     in0=xv[:, t, :, :],
                     scalar1=negmean[:],

@@ -16,12 +16,21 @@ K = 512
 C = 6
 T = 4
 ROW = K * C
+HALF = ROW // 2
 NPOS = 80 * 24
 NT = NPOS // P
 EPS = 1e-5
 HCOLS = (C + 1) * P
+XBUFS = 7
 
 FLOPS = 2 * NPOS * C * K * K + 2 * NPOS * K * K
+
+LAG_STATS = -8
+LAG_NORM = -2
+LAG_REGROUP = 4
+LAG_MX = 7
+LAG_E1 = 8
+LAG_E2 = 9
 
 
 def tile_colorresblock_t_kernel(tc, x, conv_weight, conv_bias, norm_weight, norm_bias, out):
@@ -31,18 +40,19 @@ def tile_colorresblock_t_kernel(tc, x, conv_weight, conv_bias, norm_weight, norm
 
     with ExitStack() as ctx:
         const = ctx.enter_context(tc.tile_pool(name="const", bufs=1))
-        xpool = ctx.enter_context(tc.tile_pool(name="xpool", bufs=6))
+        xpool = ctx.enter_context(tc.tile_pool(name="xpool", bufs=XBUFS))
         small = ctx.enter_context(tc.tile_pool(name="small", bufs=4))
         work = ctx.enter_context(tc.tile_pool(name="work", bufs=2))
         pst = ctx.enter_context(tc.psum_pool(name="pst", bufs=4))
         psm = ctx.enter_context(tc.psum_pool(name="psm", bufs=4))
+        ctx.enter_context(tc.manual_schedule())
 
         st = {}
 
-        def load(i):
+        def load(a):
             xt = xpool.tile([P, ROW], BF16, name="xt")
-            nc.sync.dma_start(out=xt[:], in_=xr[i * P : (i + 1) * P, :])
-            st[("x", i)] = xt
+            nc.sync.dma_start(out=xt[:], in_=xr[a * P : (a + 1) * P, :])
+            st[("x", a)] = xt
 
         load(0)
 
@@ -50,6 +60,7 @@ def tile_colorresblock_t_kernel(tc, x, conv_weight, conv_bias, norm_weight, norm
         make_identity(nc, ident[:])
         negh = const.tile([P, 1], F32, name="negh")
         nc.vector.memset(negh[:], -0.5)
+        junk = const.tile([P, HALF], BF16, name="junk")
 
         wraw = const.tile([P, 4, 2 * K], BF16, name="wraw")
         nc.sync.dma_start(out=wraw[:], in_=conv_weight.rearrange("(c p) k s -> p c (k s)", p=P))
@@ -60,6 +71,8 @@ def tile_colorresblock_t_kernel(tc, x, conv_weight, conv_bias, norm_weight, norm
         load(1)
         cbraw = const.tile([P, K], BF16, name="cbraw")
         nc.sync.dma_start(out=cbraw[:], in_=conv_bias.partition_broadcast(P))
+        for a in range(2, XBUFS):
+            load(a)
 
         gcol = const.tile([P, T], F32, name="gcol")
         nc.vector.tensor_copy(out=gcol[:], in_=graw[:])
@@ -67,15 +80,12 @@ def tile_colorresblock_t_kernel(tc, x, conv_weight, conv_bias, norm_weight, norm
         nc.vector.tensor_copy(out=bcol[:], in_=braw[:])
         b6col = const.tile([P, T], F32, name="b6col")
         nc.vector.tensor_scalar(out=b6col[:], in0=braw[:], scalar1=float(C), scalar2=None, op0=ALU.mult)
-        cb = const.tile([P, K], F32, name="cb")
-        nc.vector.tensor_copy(out=cb[:], in_=cbraw[:])
 
         wv = wraw[:].rearrange("p c (q t s) -> p c t q s", t=T, s=2)
         wf_a = const.tile([P, 4, T, P], F32, name="wf_a")
         nc.vector.tensor_tensor(out=wf_a[:], in0=wv[:, :, :, :, 0], in1=wv[:, :, :, :, 1], op=ALU.subtract)
         wf_b = const.tile([P, 4, T, P], F32, name="wf_b")
         nc.vector.tensor_copy(out=wf_b[:], in_=wv[:, :, :, :, 1])
-
         wcodes = []
         wscales = []
         for m, wf in enumerate((wf_a, wf_b)):
@@ -84,148 +94,219 @@ def tile_colorresblock_t_kernel(tc, x, conv_weight, conv_bias, norm_weight, norm
                 pw = pst.tile([P, 512], F32, name="pw", tag="pt")
                 for t in range(T):
                     nc.tensor.transpose(pw[:, t * P : (t + 1) * P], wf[:, oc, t, :], ident[:])
-                src = pw[:].rearrange("p (t o) -> p o t", t=T)
-                dst = wg[:, oc * P : (oc + 1) * P, :]
-                if oc % 2 == 0:
-                    nc.vector.tensor_copy(out=dst, in_=src)
-                else:
-                    nc.scalar.copy(out=dst, in_=src)
+                nc.vector.tensor_copy(
+                    out=wg[:, oc * P : (oc + 1) * P, :], in_=pw[:].rearrange("p (t o) -> p o t", t=T)
+                )
             wc = const.tile([P, K], U32, name="wc%d" % m, align_bytes=64)
             ws = const.tile([P, K], U8, name="ws%d" % m, align_bytes=64)
-            nc.vector.quantize_mx(
-                out=wc[:].bitcast(FP8X4), scales=ws[:], in_=wg[:].rearrange("p o t -> p (o t)")
-            )
             wcodes.append(wc)
             wscales.append(ws)
-
-        def stats(i):
-            xt = st[("x", i)]
-            junk = work.tile([P, ROW], BF16, name="junk", bufs=1)
-            sx = small.tile([P, 1], F32, name="sx")
-            nc.scalar.activation(out=junk[:], in_=xt[:], func=ACT.Identity, accum_out=sx[:])
-            negmean = small.tile([P, 1], F32, name="negmean")
-            nc.vector.tensor_scalar(out=negmean[:], in0=sx[:], scalar1=-1.0 / ROW, scalar2=None, op0=ALU.mult)
-            junk2 = work.tile([P, ROW], BF16, name="junk2", tag="junk", bufs=1)
-            ssq = small.tile([P, 1], F32, name="ssq")
-            nc.scalar.activation(
-                out=junk2[:], in_=xt[:], func=ACT.Square, bias=negmean[:], scale=1.0, accum_out=ssq[:]
+            st[("wg", m)] = wg
+        for m in range(2):
+            nc.vector.quantize_mx(
+                out=wcodes[m][:].bitcast(FP8X4),
+                scales=wscales[m][:],
+                in_=st[("wg", m)][:].rearrange("p o t -> p (o t)"),
             )
-            var = small.tile([P, 1], F32, name="var")
+        cb = const.tile([P, K], F32, name="cb")
+        nc.vector.tensor_copy(out=cb[:], in_=cbraw[:])
+
+        def stats_piece(a, i):
+            xt = st[("x", a)]
+            h = i % 2
+            cols = slice(h * HALF, (h + 1) * HALF)
+            if i == 0:
+                sx = small.tile([P, 2], F32, name="sx")
+                st[("sx", a)] = sx
+            if i == 2:
+                sq = small.tile([P, 2], F32, name="sq")
+                st[("sq", a)] = sq
+            if i < 2:
+                sx = st[("sx", a)]
+                nc.scalar.activation(out=junk[:], in_=xt[:, cols], func=ACT.Identity, accum_out=sx[:, h : h + 1])
+            else:
+                sq = st[("sq", a)]
+                nc.scalar.activation(
+                    out=junk[:], in_=xt[:, cols], func=ACT.Square, bias=st[("nm", a)][:], scale=1.0,
+                    accum_out=sq[:, h : h + 1],
+                )
+            if i == 1:
+                negmean = small.tile([P, 1], F32, name="negmean")
+                nc.gpsimd.tensor_scalar(
+                    out=negmean[:], in0=sx[:, 0:1], scalar1=sx[:, 1:2], scalar2=-1.0 / ROW,
+                    op0=ALU.add, op1=ALU.mult,
+                )
+                st[("nm", a)] = negmean
+            if i == 3:
+                var = small.tile([P, 1], F32, name="var")
+                nc.gpsimd.tensor_scalar(
+                    out=var[:], in0=sq[:, 0:1], scalar1=sq[:, 1:2], scalar2=1.0 / ROW, op0=ALU.add, op1=ALU.mult
+                )
+                vare = small.tile([P, 1], F32, name="vare")
+                nc.gpsimd.tensor_scalar(
+                    out=vare[:], in0=var[:], scalar1=1.0, scalar2=EPS, op0=ALU.mult, op1=ALU.add
+                )
+                rstd = small.tile([P, 1], F32, name="rstd")
+                nc.gpsimd.tensor_tensor(out=rstd[:], in0=vare[:], in1=negh[:], op=ALU.pow)
+                st[("rs", a)] = rstd
+
+        def norm_piece(a, t):
+            if t == 0:
+                u = work.tile([P, T, C, P], F32, name="u")
+                st[("u", a)] = u
+            u = st[("u", a)]
+            xv = st[("x", a)][:].rearrange("p (q t d) -> p t d q", t=T, d=C)
             nc.vector.tensor_scalar(
-                out=var[:], in0=ssq[:], scalar1=1.0 / ROW, scalar2=EPS, op0=ALU.mult, op1=ALU.add
+                out=u[:, t, :, :], in0=xv[:, t, :, :], scalar1=st[("nm", a)][:], scalar2=st[("rs", a)][:],
+                op0=ALU.add, op1=ALU.mult,
             )
-            rstd = small.tile([P, 1], F32, name="rstd")
-            nc.gpsimd.tensor_tensor(out=rstd[:], in0=var[:], in1=negh[:], op=ALU.pow)
-            st[("nm", i)] = negmean
-            st[("rs", i)] = rstd
 
-        def front(i):
-            xt = st[("x", i)]
-            negmean = st[("nm", i)]
-            rstd = st[("rs", i)]
-            xv = xt[:].rearrange("p (q t d) -> p t d q", t=T, d=C)
-            u = work.tile([P, T, C, P], F32, name="u")
-            ht = work.tile([P, T, HCOLS], BF16, name="ht")
-            for t in range(T):
-                nc.vector.tensor_scalar(
-                    out=u[:, t, :, :],
-                    in0=xv[:, t, :, :],
-                    scalar1=negmean[:],
-                    scalar2=rstd[:],
-                    op0=ALU.add,
-                    op1=ALU.mult,
+        def transposes(a, t):
+            u = st[("u", a)]
+            pa = pst.tile([P, 512], F32, name="pa", tag="pt")
+            for d in range(4):
+                nc.tensor.transpose(pa[:, d * P : (d + 1) * P], u[:, t, d, :], ident[:])
+            pb = pst.tile([P, 512], F32, name="pb", tag="pt")
+            for d in range(4, C):
+                nc.tensor.transpose(pb[:, (d - 4) * P : (d - 3) * P], u[:, t, d, :], ident[:])
+            for d in range(C):
+                nc.tensor.matmul(
+                    pb[:, 2 * P : 3 * P], lhsT=u[:, t, d, :], rhs=ident[:], is_transpose=True,
+                    start=(d == 0), stop=(d == C - 1),
                 )
-            for t in range(T):
-                pa = pst.tile([P, 512], F32, name="pa", tag="pt")
-                for d in range(4):
-                    nc.tensor.transpose(pa[:, d * P : (d + 1) * P], u[:, t, d, :], ident[:])
-                pb = pst.tile([P, 512], F32, name="pb", tag="pt")
-                for d in range(4, C):
-                    nc.tensor.transpose(pb[:, (d - 4) * P : (d - 3) * P], u[:, t, d, :], ident[:])
-                for d in range(C):
-                    nc.tensor.matmul(
-                        pb[:, 2 * P : 3 * P],
-                        lhsT=u[:, t, d, :],
-                        rhs=ident[:],
-                        is_transpose=True,
-                        start=(d == 0),
-                        stop=(d == C - 1),
-                    )
-                g = gcol[:, t : t + 1]
-                nc.scalar.activation(
-                    out=ht[:, t, 0 : 4 * P], in_=pa[:], func=ACT.Identity, scale=g, bias=bcol[:, t : t + 1]
-                )
-                nc.scalar.activation(
-                    out=ht[:, t, 4 * P : 6 * P], in_=pb[:, 0 : 2 * P], func=ACT.Identity, scale=g,
-                    bias=bcol[:, t : t + 1],
-                )
-                nc.scalar.activation(
-                    out=ht[:, t, 6 * P : 7 * P], in_=pb[:, 2 * P : 3 * P], func=ACT.Identity, scale=g,
-                    bias=b6col[:, t : t + 1],
-                )
-            st[("ht", i)] = ht
+            st[("pa", a, t)] = pa
+            st[("pb", a, t)] = pb
 
-        def back(i):
-            xt = st[("x", i)]
-            ht = st[("ht", i)]
-            gr = work.tile([P, HCOLS, T], BF16, name="gr", align_bytes=64)
-            nc.vector.tensor_copy(out=gr[:], in_=ht[:].rearrange("p t c -> p c t"))
-            hc = work.tile([P, HCOLS], U32, name="hc", align_bytes=64)
-            hsc = work.tile([P, HCOLS], U8, name="hsc", align_bytes=64)
-            for lo, hi in ((0, 512), (512, 768), (768, 896)):
-                nc.vector.quantize_mx(
-                    out=hc[:, lo:hi].bitcast(FP8X4),
-                    scales=hsc[:, lo:hi],
-                    in_=gr[:, lo:hi, :].rearrange("p c t -> p (c t)"),
-                )
-            tt = work.tile([P, 2, 3 * K], F32, name="tt")
+        def affine(a, t):
+            if t == 0:
+                ht = work.tile([P, T, HCOLS], BF16, name="ht")
+                st[("ht", a)] = ht
+            ht = st[("ht", a)]
+            pa = st[("pa", a, t)]
+            pb = st[("pb", a, t)]
+            g = gcol[:, t : t + 1]
+            b = bcol[:, t : t + 1]
+            nc.scalar.activation(out=ht[:, t, 0 : 4 * P], in_=pa[:], func=ACT.Identity, scale=g, bias=b)
+            nc.scalar.activation(out=ht[:, t, 4 * P : 6 * P], in_=pb[:, 0 : 2 * P], func=ACT.Identity, scale=g, bias=b)
+            nc.scalar.activation(
+                out=ht[:, t, 6 * P : 7 * P], in_=pb[:, 2 * P : 3 * P], func=ACT.Identity, scale=g,
+                bias=b6col[:, t : t + 1],
+            )
+
+        def regroup(a, lo, hi):
+            if lo == 0:
+                gr = work.tile([P, HCOLS, T], BF16, name="gr", align_bytes=64)
+                st[("gr", a)] = gr
+            gr = st[("gr", a)]
+            ht = st[("ht", a)]
+            nc.vector.tensor_copy(out=gr[:, lo:hi, :], in_=ht[:, :, lo:hi].rearrange("p t c -> p c t"))
+
+        def quantise(a, lo, hi):
+            if lo == 0:
+                hc = work.tile([P, HCOLS], U32, name="hc", align_bytes=64)
+                hsc = work.tile([P, HCOLS], U8, name="hsc", align_bytes=64)
+                st[("hc", a)] = hc
+                st[("hsc", a)] = hsc
+            nc.vector.quantize_mx(
+                out=st[("hc", a)][:, lo:hi].bitcast(FP8X4),
+                scales=st[("hsc", a)][:, lo:hi],
+                in_=st[("gr", a)][:, lo:hi, :].rearrange("p c t -> p (c t)"),
+            )
+
+        def mx(a, oc):
+            hc = st[("hc", a)]
+            hsc = st[("hsc", a)]
+            ocs = slice(oc * P, (oc + 1) * P)
             for e in range(2):
-                for oc in range(4):
-                    pm = psm.tile([P, 512], F32, name="pm")
-                    ocs = slice(oc * P, (oc + 1) * P)
-                    for j in range(3):
-                        d = 2 * j + e
-                        nc.tensor.matmul_mx(
-                            out=pm[:, j * P : (j + 1) * P],
-                            lhsT=hc[:, d * P : (d + 1) * P].bitcast(FP8X4),
-                            lhsT_scale=hsc[:, d * P : (d + 1) * P],
-                            rhs=wcodes[0][:, ocs].bitcast(FP8X4),
-                            rhs_scale=wscales[0][:, ocs],
-                            start=True,
-                            stop=False,
-                        )
-                        nc.tensor.matmul_mx(
-                            out=pm[:, j * P : (j + 1) * P],
-                            lhsT=hc[:, C * P : (C + 1) * P].bitcast(FP8X4),
-                            lhsT_scale=hsc[:, C * P : (C + 1) * P],
-                            rhs=wcodes[1][:, ocs].bitcast(FP8X4),
-                            rhs_scale=wscales[1][:, ocs],
-                            start=False,
-                            stop=True,
-                        )
-                    nc.vector.tensor_tensor(
-                        out=tt[:, e, oc * 3 * P : (oc + 1) * 3 * P].rearrange("p (o j) -> p o j", j=3),
-                        in0=pm[:, 0 : 3 * P].rearrange("p (j o) -> p o j", j=3),
-                        in1=cb[:, ocs].unsqueeze(2).to_broadcast([P, P, 3]),
-                        op=ALU.add,
+                pm = psm.tile([P, 512], F32, name="pm")
+                for j in range(3):
+                    d = 2 * j + e
+                    nc.tensor.matmul_mx(
+                        out=pm[:, j * P : (j + 1) * P],
+                        lhsT=hc[:, d * P : (d + 1) * P].bitcast(FP8X4),
+                        lhsT_scale=hsc[:, d * P : (d + 1) * P],
+                        rhs=wcodes[0][:, ocs].bitcast(FP8X4),
+                        rhs_scale=wscales[0][:, ocs],
+                        start=True,
+                        stop=False,
                     )
-            ot = work.tile([P, ROW], F32, name="ot")
+                    nc.tensor.matmul_mx(
+                        out=pm[:, j * P : (j + 1) * P],
+                        lhsT=hc[:, C * P : (C + 1) * P].bitcast(FP8X4),
+                        lhsT_scale=hsc[:, C * P : (C + 1) * P],
+                        rhs=wcodes[1][:, ocs].bitcast(FP8X4),
+                        rhs_scale=wscales[1][:, ocs],
+                        start=False,
+                        stop=True,
+                    )
+                st[("pm", a, oc, e)] = pm
+
+        def e1(a, oc):
+            if oc == 0:
+                tt = work.tile([P, 2, 3 * K], F32, name="tt")
+                st[("tt", a)] = tt
+            tt = st[("tt", a)]
+            for e in range(2):
+                pm = st[("pm", a, oc, e)]
+                nc.vector.tensor_tensor(
+                    out=tt[:, e, oc * 3 * P : (oc + 1) * 3 * P].rearrange("p (o j) -> p o j", j=3),
+                    in0=pm[:, 0 : 3 * P].rearrange("p (j o) -> p o j", j=3),
+                    in1=cb[:, oc * P : (oc + 1) * P].unsqueeze(2).to_broadcast([P, P, 3]),
+                    op=ALU.add,
+                )
+
+        def e2(a, oc):
+            if oc == 0:
+                ot = work.tile([P, ROW], F32, name="ot")
+                st[("ot", a)] = ot
+            ot = st[("ot", a)]
+            tt = st[("tt", a)]
+            xt = st[("x", a)]
+            cols = slice(oc * C * P, (oc + 1) * C * P)
             nc.vector.scalar_tensor_tensor(
-                out=ot[:].rearrange("p (a e) -> p a e", e=2),
-                in0=tt[:].rearrange("p e a -> p a e"),
+                out=ot[:, cols].rearrange("p (a e) -> p a e", e=2),
+                in0=tt[:, :, oc * 3 * P : (oc + 1) * 3 * P].rearrange("p e a -> p a e"),
                 scalar=0.0,
-                in1=xt[:].rearrange("p (a e) -> p a e", e=2),
+                in1=xt[:, cols].rearrange("p (a e) -> p a e", e=2),
                 op0=ALU.max,
                 op1=ALU.add,
             )
-            nc.sync.dma_start(out=outr[i * P : (i + 1) * P, :], in_=ot[:])
+            if oc % 2 == 1:
+                hcols = slice((oc - 1) * C * P, (oc + 1) * C * P)
+                nc.sync.dma_start(out=outr[a * P : (a + 1) * P, hcols], in_=ot[:, hcols])
 
-        for n in range(NT + 2):
-            if n + 2 < NT:
-                load(n + 2)
-            if n < NT:
-                stats(n)
-            if 0 <= n - 2:
-                back(n - 2)
-            if 0 <= n - 1 < NT:
-                front(n - 1)
+        def piece(g, lag):
+            a, r = divmod(g - lag, 4)
+            return (a, r) if 0 <= a < NT else None
+
+        for g in range(LAG_STATS, 4 * (NT - 1) + LAG_E2 + 4):
+            w = piece(g, LAG_STATS)
+            if w:
+                stats_piece(w[0], w[1])
+            w = piece(g, LAG_E1)
+            if w:
+                e1(w[0], w[1])
+            w = piece(g, 0)
+            if w:
+                transposes(w[0], w[1])
+                affine(w[0], w[1])
+            w = piece(g, LAG_REGROUP)
+            if w and w[1] == 0:
+                regroup(w[0], 0, 512)
+            if w and w[1] == 1:
+                quantise(w[0], 0, 512)
+                regroup(w[0], 512, 896)
+            w2 = piece(g, LAG_E2)
+            if w2:
+                e2(w2[0], w2[1])
+                if w2[1] == 3 and w2[0] + XBUFS < NT:
+                    load(w2[0] + XBUFS)
+            if w and w[1] == 2:
+                quantise(w[0], 512, 768)
+                quantise(w[0], 768, 896)
+            w = piece(g, LAG_NORM)
+            if w:
+                norm_piece(w[0], w[1])
+            w = piece(g, LAG_MX)
+            if w:
+                mx(w[0], w[1])

@@ -21,11 +21,13 @@ NPOS = 80 * 24
 NT = NPOS // P
 EPS = 1e-5
 HCOLS = (C + 1) * P
-XBUFS = 7
+XBUFS = 8
+RAW_SUM_TILES = 2
 
 FLOPS = 2 * NPOS * C * K * K + 2 * NPOS * K * K
 
-LAG_STATS = -8
+LAG_XS = -14
+LAG_STATS = -9
 LAG_NORM = -2
 LAG_REGROUP = 4
 LAG_MX = 7
@@ -86,6 +88,7 @@ def tile_colorresblock_t_kernel(tc, x, conv_weight, conv_bias, norm_weight, norm
         nc.vector.tensor_tensor(out=wf_a[:], in0=wv[:, :, :, :, 0], in1=wv[:, :, :, :, 1], op=ALU.subtract)
         wf_b = const.tile([P, 4, T, P], F32, name="wf_b")
         nc.vector.tensor_copy(out=wf_b[:], in_=wv[:, :, :, :, 1])
+
         wcodes = []
         wscales = []
         for m, wf in enumerate((wf_a, wf_b)):
@@ -111,10 +114,31 @@ def tile_colorresblock_t_kernel(tc, x, conv_weight, conv_bias, norm_weight, norm
         cb = const.tile([P, K], F32, name="cb")
         nc.vector.tensor_copy(out=cb[:], in_=cbraw[:])
 
+        def colour_sum_piece(a, i):
+            xd = st[("x", a)][:].rearrange("p (k d) -> p d k", d=C)
+            if i == 0:
+                s01 = work.tile([P, K], F32, name="s01")
+                nc.gpsimd.tensor_tensor(out=s01[:], in0=xd[:, 0, :], in1=xd[:, 1, :], op=ALU.add)
+                s23 = work.tile([P, K], F32, name="s23")
+                nc.gpsimd.tensor_tensor(out=s23[:], in0=xd[:, 2, :], in1=xd[:, 3, :], op=ALU.add)
+                st[("s01", a)] = s01
+                st[("s23", a)] = s23
+            if i == 1:
+                s45 = work.tile([P, K], F32, name="s45")
+                nc.gpsimd.tensor_tensor(out=s45[:], in0=xd[:, 4, :], in1=xd[:, 5, :], op=ALU.add)
+                st[("s45", a)] = s45
+            if i == 2:
+                s01 = st[("s01", a)]
+                nc.gpsimd.tensor_tensor(out=s01[:], in0=s01[:], in1=st[("s23", a)][:], op=ALU.add)
+            if i == 3:
+                s01 = st[("s01", a)]
+                nc.gpsimd.tensor_tensor(out=s01[:], in0=s01[:], in1=st[("s45", a)][:], op=ALU.add)
+
         def stats_piece(a, i):
             xt = st[("x", a)]
             h = i % 2
             cols = slice(h * HALF, (h + 1) * HALF)
+            raw = a < RAW_SUM_TILES
             if i == 0:
                 sx = small.tile([P, 2], F32, name="sx")
                 st[("sx", a)] = sx
@@ -123,20 +147,38 @@ def tile_colorresblock_t_kernel(tc, x, conv_weight, conv_bias, norm_weight, norm
                 st[("sq", a)] = sq
             if i < 2:
                 sx = st[("sx", a)]
-                nc.scalar.activation(out=junk[:], in_=xt[:, cols], func=ACT.Identity, accum_out=sx[:, h : h + 1])
+                if raw:
+                    nc.scalar.activation(
+                        out=junk[:], in_=xt[:, cols], func=ACT.Identity, accum_out=sx[:, h : h + 1]
+                    )
+                elif i == 0:
+                    nc.scalar.activation(
+                        out=junk[:, 0:K], in_=st[("s01", a)][:], func=ACT.Identity, accum_out=sx[:, 0:1]
+                    )
             else:
                 sq = st[("sq", a)]
                 nc.scalar.activation(
                     out=junk[:], in_=xt[:, cols], func=ACT.Square, bias=st[("nm", a)][:], scale=1.0,
                     accum_out=sq[:, h : h + 1],
                 )
-            if i == 1:
+            if i == (1 if raw else 0):
                 negmean = small.tile([P, 1], F32, name="negmean")
+                if raw:
+                    nc.gpsimd.tensor_scalar(
+                        out=negmean[:], in0=sx[:, 0:1], scalar1=sx[:, 1:2], scalar2=-1.0 / ROW,
+                        op0=ALU.add, op1=ALU.mult,
+                    )
+                else:
+                    nc.gpsimd.tensor_scalar(
+                        out=negmean[:], in0=sx[:, 0:1], scalar1=-1.0 / ROW, scalar2=0.0,
+                        op0=ALU.mult, op1=ALU.add,
+                    )
+                negmean6 = small.tile([P, 1], F32, name="negmean6")
                 nc.gpsimd.tensor_scalar(
-                    out=negmean[:], in0=sx[:, 0:1], scalar1=sx[:, 1:2], scalar2=-1.0 / ROW,
-                    op0=ALU.add, op1=ALU.mult,
+                    out=negmean6[:], in0=negmean[:], scalar1=float(C), scalar2=0.0, op0=ALU.mult, op1=ALU.add
                 )
                 st[("nm", a)] = negmean
+                st[("nm6", a)] = negmean6
             if i == 3:
                 var = small.tile([P, 1], F32, name="var")
                 nc.gpsimd.tensor_scalar(
@@ -149,6 +191,13 @@ def tile_colorresblock_t_kernel(tc, x, conv_weight, conv_bias, norm_weight, norm
                 rstd = small.tile([P, 1], F32, name="rstd")
                 nc.gpsimd.tensor_tensor(out=rstd[:], in0=vare[:], in1=negh[:], op=ALU.pow)
                 st[("rs", a)] = rstd
+                if not raw:
+                    us = work.tile([P, T, P], F32, name="us")
+                    nc.gpsimd.tensor_scalar(
+                        out=us[:], in0=st[("s01", a)][:].rearrange("p (q t) -> p t q", t=T),
+                        scalar1=st[("nm6", a)][:], scalar2=rstd[:], op0=ALU.add, op1=ALU.mult,
+                    )
+                    st[("us", a)] = us
 
         def norm_piece(a, t):
             if t == 0:
@@ -169,11 +218,14 @@ def tile_colorresblock_t_kernel(tc, x, conv_weight, conv_bias, norm_weight, norm
             pb = pst.tile([P, 512], F32, name="pb", tag="pt")
             for d in range(4, C):
                 nc.tensor.transpose(pb[:, (d - 4) * P : (d - 3) * P], u[:, t, d, :], ident[:])
-            for d in range(C):
-                nc.tensor.matmul(
-                    pb[:, 2 * P : 3 * P], lhsT=u[:, t, d, :], rhs=ident[:], is_transpose=True,
-                    start=(d == 0), stop=(d == C - 1),
-                )
+            if a < RAW_SUM_TILES:
+                for d in range(C):
+                    nc.tensor.matmul(
+                        pb[:, 2 * P : 3 * P], lhsT=u[:, t, d, :], rhs=ident[:], is_transpose=True,
+                        start=(d == 0), stop=(d == C - 1),
+                    )
+            else:
+                nc.tensor.transpose(pb[:, 2 * P : 3 * P], st[("us", a)][:, t, :], ident[:])
             st[("pa", a, t)] = pa
             st[("pb", a, t)] = pb
 
@@ -213,33 +265,35 @@ def tile_colorresblock_t_kernel(tc, x, conv_weight, conv_bias, norm_weight, norm
                 in_=st[("gr", a)][:, lo:hi, :].rearrange("p c t -> p (c t)"),
             )
 
-        def mx(a, oc):
+        def mx_pass(a, dst, d, m, ocs):
             hc = st[("hc", a)]
             hsc = st[("hsc", a)]
+            nc.tensor.matmul_mx(
+                out=dst,
+                lhsT=hc[:, d * P : (d + 1) * P].bitcast(FP8X4),
+                lhsT_scale=hsc[:, d * P : (d + 1) * P],
+                rhs=wcodes[m][:, ocs].bitcast(FP8X4),
+                rhs_scale=wscales[m][:, ocs],
+                start=True,
+                stop=True,
+            )
+
+        def mx(a, oc):
             ocs = slice(oc * P, (oc + 1) * P)
             for e in range(2):
                 pm = psm.tile([P, 512], F32, name="pm")
+                if e == 0:
+                    mx_pass(a, pm[:, 3 * P : 4 * P], C, 1, ocs)
                 for j in range(3):
-                    d = 2 * j + e
-                    nc.tensor.matmul_mx(
-                        out=pm[:, j * P : (j + 1) * P],
-                        lhsT=hc[:, d * P : (d + 1) * P].bitcast(FP8X4),
-                        lhsT_scale=hsc[:, d * P : (d + 1) * P],
-                        rhs=wcodes[0][:, ocs].bitcast(FP8X4),
-                        rhs_scale=wscales[0][:, ocs],
-                        start=True,
-                        stop=False,
-                    )
-                    nc.tensor.matmul_mx(
-                        out=pm[:, j * P : (j + 1) * P],
-                        lhsT=hc[:, C * P : (C + 1) * P].bitcast(FP8X4),
-                        lhsT_scale=hsc[:, C * P : (C + 1) * P],
-                        rhs=wcodes[1][:, ocs].bitcast(FP8X4),
-                        rhs_scale=wscales[1][:, ocs],
-                        start=False,
-                        stop=True,
-                    )
+                    mx_pass(a, pm[:, j * P : (j + 1) * P], 2 * j + e, 0, ocs)
                 st[("pm", a, oc, e)] = pm
+
+        def second_term(a, oc):
+            cc = work.tile([P, P], F32, name="cc")
+            nc.vector.tensor_tensor(
+                out=cc[:], in0=st[("pm", a, oc, 0)][:, 3 * P : 4 * P], in1=cb[:, oc * P : (oc + 1) * P], op=ALU.add
+            )
+            st[("cc", a, oc)] = cc
 
         def e1(a, oc):
             if oc == 0:
@@ -251,7 +305,7 @@ def tile_colorresblock_t_kernel(tc, x, conv_weight, conv_bias, norm_weight, norm
                 nc.vector.tensor_tensor(
                     out=tt[:, e, oc * 3 * P : (oc + 1) * 3 * P].rearrange("p (o j) -> p o j", j=3),
                     in0=pm[:, 0 : 3 * P].rearrange("p (j o) -> p o j", j=3),
-                    in1=cb[:, oc * P : (oc + 1) * P].unsqueeze(2).to_broadcast([P, P, 3]),
+                    in1=st[("cc", a, oc)][:].unsqueeze(2).to_broadcast([P, P, 3]),
                     op=ALU.add,
                 )
 
@@ -283,24 +337,29 @@ def tile_colorresblock_t_kernel(tc, x, conv_weight, conv_bias, norm_weight, norm
             w = piece(g, LAG_STATS)
             if w:
                 stats_piece(w[0], w[1])
-            w = piece(g, LAG_E1)
-            if w:
-                e1(w[0], w[1])
+            w = piece(g, LAG_XS)
+            if w and w[0] >= RAW_SUM_TILES:
+                colour_sum_piece(w[0], w[1])
+            w1 = piece(g, LAG_E1)
+            if w1:
+                second_term(w1[0], w1[1])
             w = piece(g, 0)
             if w:
                 transposes(w[0], w[1])
                 affine(w[0], w[1])
+            w2 = piece(g, LAG_E2)
+            if w2:
+                e2(w2[0], w2[1])
+                if w2[1] == 3 and w2[0] + XBUFS < NT:
+                    load(w2[0] + XBUFS)
+            if w1:
+                e1(w1[0], w1[1])
             w = piece(g, LAG_REGROUP)
             if w and w[1] == 0:
                 regroup(w[0], 0, 512)
             if w and w[1] == 1:
                 quantise(w[0], 0, 512)
                 regroup(w[0], 512, 896)
-            w2 = piece(g, LAG_E2)
-            if w2:
-                e2(w2[0], w2[1])
-                if w2[1] == 3 and w2[0] + XBUFS < NT:
-                    load(w2[0] + XBUFS)
             if w and w[1] == 2:
                 quantise(w[0], 512, 768)
                 quantise(w[0], 768, 896)

@@ -21,13 +21,12 @@ NPOS = 80 * 24
 NT = NPOS // P
 EPS = 1e-5
 HCOLS = (C + 1) * P
-XBUFS = 8
-RAW_SUM_TILES = 2
+XBUFS = 7
+UBUFS = 4
 
 FLOPS = 2 * NPOS * C * K * K + 2 * NPOS * K * K
 
-LAG_XS = -14
-LAG_STATS = -9
+LAG_STATS = -8
 LAG_NORM = -2
 LAG_REGROUP = 4
 LAG_MX = 7
@@ -63,6 +62,9 @@ def tile_colorresblock_t_kernel(tc, x, conv_weight, conv_bias, norm_weight, norm
         negh = const.tile([P, 1], F32, name="negh")
         nc.vector.memset(negh[:], -0.5)
         junk = const.tile([P, HALF], BF16, name="junk")
+        junk2 = const.tile([P, 2], F32, name="junk2")
+        halfeps = const.tile([P, 1], F32, name="halfeps")
+        nc.vector.memset(halfeps[:], EPS / 2.0)
 
         wraw = const.tile([P, 4, 2 * K], BF16, name="wraw")
         nc.sync.dma_start(out=wraw[:], in_=conv_weight.rearrange("(c p) k s -> p c (k s)", p=P))
@@ -88,7 +90,6 @@ def tile_colorresblock_t_kernel(tc, x, conv_weight, conv_bias, norm_weight, norm
         nc.vector.tensor_tensor(out=wf_a[:], in0=wv[:, :, :, :, 0], in1=wv[:, :, :, :, 1], op=ALU.subtract)
         wf_b = const.tile([P, 4, T, P], F32, name="wf_b")
         nc.vector.tensor_copy(out=wf_b[:], in_=wv[:, :, :, :, 1])
-
         wcodes = []
         wscales = []
         for m, wf in enumerate((wf_a, wf_b)):
@@ -114,31 +115,10 @@ def tile_colorresblock_t_kernel(tc, x, conv_weight, conv_bias, norm_weight, norm
         cb = const.tile([P, K], F32, name="cb")
         nc.vector.tensor_copy(out=cb[:], in_=cbraw[:])
 
-        def colour_sum_piece(a, i):
-            xd = st[("x", a)][:].rearrange("p (k d) -> p d k", d=C)
-            if i == 0:
-                s01 = work.tile([P, K], F32, name="s01")
-                nc.gpsimd.tensor_tensor(out=s01[:], in0=xd[:, 0, :], in1=xd[:, 1, :], op=ALU.add)
-                s23 = work.tile([P, K], F32, name="s23")
-                nc.gpsimd.tensor_tensor(out=s23[:], in0=xd[:, 2, :], in1=xd[:, 3, :], op=ALU.add)
-                st[("s01", a)] = s01
-                st[("s23", a)] = s23
-            if i == 1:
-                s45 = work.tile([P, K], F32, name="s45")
-                nc.gpsimd.tensor_tensor(out=s45[:], in0=xd[:, 4, :], in1=xd[:, 5, :], op=ALU.add)
-                st[("s45", a)] = s45
-            if i == 2:
-                s01 = st[("s01", a)]
-                nc.gpsimd.tensor_tensor(out=s01[:], in0=s01[:], in1=st[("s23", a)][:], op=ALU.add)
-            if i == 3:
-                s01 = st[("s01", a)]
-                nc.gpsimd.tensor_tensor(out=s01[:], in0=s01[:], in1=st[("s45", a)][:], op=ALU.add)
-
         def stats_piece(a, i):
             xt = st[("x", a)]
             h = i % 2
             cols = slice(h * HALF, (h + 1) * HALF)
-            raw = a < RAW_SUM_TILES
             if i == 0:
                 sx = small.tile([P, 2], F32, name="sx")
                 st[("sx", a)] = sx
@@ -147,38 +127,20 @@ def tile_colorresblock_t_kernel(tc, x, conv_weight, conv_bias, norm_weight, norm
                 st[("sq", a)] = sq
             if i < 2:
                 sx = st[("sx", a)]
-                if raw:
-                    nc.scalar.activation(
-                        out=junk[:], in_=xt[:, cols], func=ACT.Identity, accum_out=sx[:, h : h + 1]
-                    )
-                elif i == 0:
-                    nc.scalar.activation(
-                        out=junk[:, 0:K], in_=st[("s01", a)][:], func=ACT.Identity, accum_out=sx[:, 0:1]
-                    )
+                nc.scalar.activation(out=junk[:], in_=xt[:, cols], func=ACT.Identity, accum_out=sx[:, h : h + 1])
             else:
                 sq = st[("sq", a)]
                 nc.scalar.activation(
                     out=junk[:], in_=xt[:, cols], func=ACT.Square, bias=st[("nm", a)][:], scale=1.0,
                     accum_out=sq[:, h : h + 1],
                 )
-            if i == (1 if raw else 0):
+            if i == 1:
                 negmean = small.tile([P, 1], F32, name="negmean")
-                if raw:
-                    nc.gpsimd.tensor_scalar(
-                        out=negmean[:], in0=sx[:, 0:1], scalar1=sx[:, 1:2], scalar2=-1.0 / ROW,
-                        op0=ALU.add, op1=ALU.mult,
-                    )
-                else:
-                    nc.gpsimd.tensor_scalar(
-                        out=negmean[:], in0=sx[:, 0:1], scalar1=-1.0 / ROW, scalar2=0.0,
-                        op0=ALU.mult, op1=ALU.add,
-                    )
-                negmean6 = small.tile([P, 1], F32, name="negmean6")
                 nc.gpsimd.tensor_scalar(
-                    out=negmean6[:], in0=negmean[:], scalar1=float(C), scalar2=0.0, op0=ALU.mult, op1=ALU.add
+                    out=negmean[:], in0=sx[:, 0:1], scalar1=sx[:, 1:2], scalar2=-1.0 / ROW,
+                    op0=ALU.add, op1=ALU.mult,
                 )
                 st[("nm", a)] = negmean
-                st[("nm6", a)] = negmean6
             if i == 3:
                 var = small.tile([P, 1], F32, name="var")
                 nc.gpsimd.tensor_scalar(
@@ -191,13 +153,6 @@ def tile_colorresblock_t_kernel(tc, x, conv_weight, conv_bias, norm_weight, norm
                 rstd = small.tile([P, 1], F32, name="rstd")
                 nc.gpsimd.tensor_tensor(out=rstd[:], in0=vare[:], in1=negh[:], op=ALU.pow)
                 st[("rs", a)] = rstd
-                if not raw:
-                    us = work.tile([P, T, P], F32, name="us")
-                    nc.gpsimd.tensor_scalar(
-                        out=us[:], in0=st[("s01", a)][:].rearrange("p (q t) -> p t q", t=T),
-                        scalar1=st[("nm6", a)][:], scalar2=rstd[:], op0=ALU.add, op1=ALU.mult,
-                    )
-                    st[("us", a)] = us
 
         def norm_piece(a, t):
             if t == 0:
@@ -210,6 +165,53 @@ def tile_colorresblock_t_kernel(tc, x, conv_weight, conv_bias, norm_weight, norm
                 op0=ALU.add, op1=ALU.mult,
             )
 
+        def stats_piece(a, i):
+            xt = st[("x", a)]
+            h = i % 2
+            if i == 0:
+                sx = small.tile([P, 2], F32, name="sx")
+                st[("sx", a)] = sx
+                u = work.tile([P, T, C, P], F32, name="u", bufs=UBUFS)
+                st[("u", a)] = u
+            if i == 2:
+                sq = small.tile([P, 2], F32, name="sq")
+                st[("sq", a)] = sq
+            if i < 2:
+                xv = xt[:].rearrange("p (q t d) -> p t d q", t=T, d=C)
+                nc.scalar.activation(
+                    out=st[("u", a)][:, 2 * h : 2 * h + 2, :, :], in_=xv[:, 2 * h : 2 * h + 2, :, :],
+                    func=ACT.Identity, accum_out=st[("sx", a)][:, h : h + 1],
+                )
+            else:
+                nc.scalar.activation(
+                    out=junk[:], in_=xt[:, h * HALF : (h + 1) * HALF], func=ACT.Square, bias=st[("nm", a)][:],
+                    scale=1.0, accum_out=st[("sq", a)][:, h : h + 1],
+                )
+
+        def stats_small(a, i):
+            if i == 2:
+                negmean = small.tile([P, 1], F32, name="negmean")
+                nc.scalar.activation(
+                    out=junk2[:], in_=st[("sx", a)][:], func=ACT.Identity, scale=-1.0 / ROW, accum_out=negmean[:]
+                )
+                st[("nm", a)] = negmean
+            if i == 4:
+                vare = small.tile([P, 1], F32, name="vare")
+                nc.scalar.activation(
+                    out=junk2[:], in_=st[("sq", a)][:], func=ACT.Identity, scale=1.0 / ROW, bias=halfeps[:],
+                    accum_out=vare[:],
+                )
+                rstd = small.tile([P, 1], F32, name="rstd")
+                nc.gpsimd.tensor_tensor(out=rstd[:], in0=vare[:], in1=negh[:], op=ALU.pow)
+                st[("rs", a)] = rstd
+
+        def norm_piece(a, t):
+            u = st[("u", a)]
+            nc.vector.tensor_scalar(
+                out=u[:, t, :, :], in0=u[:, t, :, :], scalar1=st[("nm", a)][:], scalar2=st[("rs", a)][:],
+                op0=ALU.add, op1=ALU.mult,
+            )
+
         def transposes(a, t):
             u = st[("u", a)]
             pa = pst.tile([P, 512], F32, name="pa", tag="pt")
@@ -218,14 +220,11 @@ def tile_colorresblock_t_kernel(tc, x, conv_weight, conv_bias, norm_weight, norm
             pb = pst.tile([P, 512], F32, name="pb", tag="pt")
             for d in range(4, C):
                 nc.tensor.transpose(pb[:, (d - 4) * P : (d - 3) * P], u[:, t, d, :], ident[:])
-            if a < RAW_SUM_TILES:
-                for d in range(C):
-                    nc.tensor.matmul(
-                        pb[:, 2 * P : 3 * P], lhsT=u[:, t, d, :], rhs=ident[:], is_transpose=True,
-                        start=(d == 0), stop=(d == C - 1),
-                    )
-            else:
-                nc.tensor.transpose(pb[:, 2 * P : 3 * P], st[("us", a)][:, t, :], ident[:])
+            for d in range(C):
+                nc.tensor.matmul(
+                    pb[:, 2 * P : 3 * P], lhsT=u[:, t, d, :], rhs=ident[:], is_transpose=True,
+                    start=(d == 0), stop=(d == C - 1),
+                )
             st[("pa", a, t)] = pa
             st[("pb", a, t)] = pb
 
@@ -251,7 +250,10 @@ def tile_colorresblock_t_kernel(tc, x, conv_weight, conv_bias, norm_weight, norm
                 st[("gr", a)] = gr
             gr = st[("gr", a)]
             ht = st[("ht", a)]
-            nc.vector.tensor_copy(out=gr[:, lo:hi, :], in_=ht[:, :, lo:hi].rearrange("p t c -> p c t"))
+            nc.vector.tensor_copy(
+                out=gr[:, lo:hi, :].rearrange("p (c i) t -> p c t i", i=4),
+                in_=ht[:, :, lo:hi].rearrange("p t (c i) -> p c t i", i=4),
+            )
 
         def quantise(a, lo, hi):
             if lo == 0:
@@ -265,35 +267,33 @@ def tile_colorresblock_t_kernel(tc, x, conv_weight, conv_bias, norm_weight, norm
                 in_=st[("gr", a)][:, lo:hi, :].rearrange("p c t -> p (c t)"),
             )
 
-        def mx_pass(a, dst, d, m, ocs):
+        def mx(a, oc):
             hc = st[("hc", a)]
             hsc = st[("hsc", a)]
-            nc.tensor.matmul_mx(
-                out=dst,
-                lhsT=hc[:, d * P : (d + 1) * P].bitcast(FP8X4),
-                lhsT_scale=hsc[:, d * P : (d + 1) * P],
-                rhs=wcodes[m][:, ocs].bitcast(FP8X4),
-                rhs_scale=wscales[m][:, ocs],
-                start=True,
-                stop=True,
-            )
-
-        def mx(a, oc):
             ocs = slice(oc * P, (oc + 1) * P)
             for e in range(2):
                 pm = psm.tile([P, 512], F32, name="pm")
-                if e == 0:
-                    mx_pass(a, pm[:, 3 * P : 4 * P], C, 1, ocs)
                 for j in range(3):
-                    mx_pass(a, pm[:, j * P : (j + 1) * P], 2 * j + e, 0, ocs)
+                    d = 2 * j + e
+                    nc.tensor.matmul_mx(
+                        out=pm[:, j * P : (j + 1) * P],
+                        lhsT=hc[:, d * P : (d + 1) * P].bitcast(FP8X4),
+                        lhsT_scale=hsc[:, d * P : (d + 1) * P],
+                        rhs=wcodes[0][:, ocs].bitcast(FP8X4),
+                        rhs_scale=wscales[0][:, ocs],
+                        start=True,
+                        stop=False,
+                    )
+                    nc.tensor.matmul_mx(
+                        out=pm[:, j * P : (j + 1) * P],
+                        lhsT=hc[:, C * P : (C + 1) * P].bitcast(FP8X4),
+                        lhsT_scale=hsc[:, C * P : (C + 1) * P],
+                        rhs=wcodes[1][:, ocs].bitcast(FP8X4),
+                        rhs_scale=wscales[1][:, ocs],
+                        start=False,
+                        stop=True,
+                    )
                 st[("pm", a, oc, e)] = pm
-
-        def second_term(a, oc):
-            cc = work.tile([P, P], F32, name="cc")
-            nc.vector.tensor_tensor(
-                out=cc[:], in0=st[("pm", a, oc, 0)][:, 3 * P : 4 * P], in1=cb[:, oc * P : (oc + 1) * P], op=ALU.add
-            )
-            st[("cc", a, oc)] = cc
 
         def e1(a, oc):
             if oc == 0:
@@ -305,7 +305,7 @@ def tile_colorresblock_t_kernel(tc, x, conv_weight, conv_bias, norm_weight, norm
                 nc.vector.tensor_tensor(
                     out=tt[:, e, oc * 3 * P : (oc + 1) * 3 * P].rearrange("p (o j) -> p o j", j=3),
                     in0=pm[:, 0 : 3 * P].rearrange("p (j o) -> p o j", j=3),
-                    in1=st[("cc", a, oc)][:].unsqueeze(2).to_broadcast([P, P, 3]),
+                    in1=cb[:, oc * P : (oc + 1) * P].unsqueeze(2).to_broadcast([P, P, 3]),
                     op=ALU.add,
                 )
 
@@ -334,32 +334,31 @@ def tile_colorresblock_t_kernel(tc, x, conv_weight, conv_bias, norm_weight, norm
             return (a, r) if 0 <= a < NT else None
 
         for g in range(LAG_STATS, 4 * (NT - 1) + LAG_E2 + 4):
-            w = piece(g, LAG_STATS)
+            for i in (2, 4):
+                w = piece(g - i, LAG_STATS)
+                if w and w[1] == 0:
+                    stats_small(w[0], i)
+            w = piece(g, LAG_E1)
             if w:
-                stats_piece(w[0], w[1])
-            w = piece(g, LAG_XS)
-            if w and w[0] >= RAW_SUM_TILES:
-                colour_sum_piece(w[0], w[1])
-            w1 = piece(g, LAG_E1)
-            if w1:
-                second_term(w1[0], w1[1])
+                e1(w[0], w[1])
             w = piece(g, 0)
             if w:
                 transposes(w[0], w[1])
                 affine(w[0], w[1])
-            w2 = piece(g, LAG_E2)
-            if w2:
-                e2(w2[0], w2[1])
-                if w2[1] == 3 and w2[0] + XBUFS < NT:
-                    load(w2[0] + XBUFS)
-            if w1:
-                e1(w1[0], w1[1])
+            w = piece(g, LAG_STATS)
+            if w:
+                stats_piece(w[0], w[1])
             w = piece(g, LAG_REGROUP)
             if w and w[1] == 0:
                 regroup(w[0], 0, 512)
             if w and w[1] == 1:
                 quantise(w[0], 0, 512)
                 regroup(w[0], 512, 896)
+            w2 = piece(g, LAG_E2)
+            if w2:
+                e2(w2[0], w2[1])
+                if w2[1] == 3 and w2[0] + XBUFS < NT:
+                    load(w2[0] + XBUFS)
             if w and w[1] == 2:
                 quantise(w[0], 512, 768)
                 quantise(w[0], 768, 896)

@@ -22,7 +22,6 @@ NT = NPOS // P
 EPS = 1e-5
 HCOLS = (C + 1) * P
 XBUFS = 7
-UBUFS = 4
 
 FLOPS = 2 * NPOS * C * K * K + 2 * NPOS * K * K
 
@@ -62,9 +61,6 @@ def tile_colorresblock_t_kernel(tc, x, conv_weight, conv_bias, norm_weight, norm
         negh = const.tile([P, 1], F32, name="negh")
         nc.vector.memset(negh[:], -0.5)
         junk = const.tile([P, HALF], BF16, name="junk")
-        junk2 = const.tile([P, 2], F32, name="junk2")
-        halfeps = const.tile([P, 1], F32, name="halfeps")
-        nc.vector.memset(halfeps[:], EPS / 2.0)
 
         wraw = const.tile([P, 4, 2 * K], BF16, name="wraw")
         nc.sync.dma_start(out=wraw[:], in_=conv_weight.rearrange("(c p) k s -> p c (k s)", p=P))
@@ -165,53 +161,6 @@ def tile_colorresblock_t_kernel(tc, x, conv_weight, conv_bias, norm_weight, norm
                 op0=ALU.add, op1=ALU.mult,
             )
 
-        def stats_piece(a, i):
-            xt = st[("x", a)]
-            h = i % 2
-            if i == 0:
-                sx = small.tile([P, 2], F32, name="sx")
-                st[("sx", a)] = sx
-                u = work.tile([P, T, C, P], F32, name="u", bufs=UBUFS)
-                st[("u", a)] = u
-            if i == 2:
-                sq = small.tile([P, 2], F32, name="sq")
-                st[("sq", a)] = sq
-            if i < 2:
-                xv = xt[:].rearrange("p (q t d) -> p t d q", t=T, d=C)
-                nc.scalar.activation(
-                    out=st[("u", a)][:, 2 * h : 2 * h + 2, :, :], in_=xv[:, 2 * h : 2 * h + 2, :, :],
-                    func=ACT.Identity, accum_out=st[("sx", a)][:, h : h + 1],
-                )
-            else:
-                nc.scalar.activation(
-                    out=junk[:], in_=xt[:, h * HALF : (h + 1) * HALF], func=ACT.Square, bias=st[("nm", a)][:],
-                    scale=1.0, accum_out=st[("sq", a)][:, h : h + 1],
-                )
-
-        def stats_small(a, i):
-            if i == 2:
-                negmean = small.tile([P, 1], F32, name="negmean")
-                nc.scalar.activation(
-                    out=junk2[:], in_=st[("sx", a)][:], func=ACT.Identity, scale=-1.0 / ROW, accum_out=negmean[:]
-                )
-                st[("nm", a)] = negmean
-            if i == 4:
-                vare = small.tile([P, 1], F32, name="vare")
-                nc.scalar.activation(
-                    out=junk2[:], in_=st[("sq", a)][:], func=ACT.Identity, scale=1.0 / ROW, bias=halfeps[:],
-                    accum_out=vare[:],
-                )
-                rstd = small.tile([P, 1], F32, name="rstd")
-                nc.gpsimd.tensor_tensor(out=rstd[:], in0=vare[:], in1=negh[:], op=ALU.pow)
-                st[("rs", a)] = rstd
-
-        def norm_piece(a, t):
-            u = st[("u", a)]
-            nc.vector.tensor_scalar(
-                out=u[:, t, :, :], in0=u[:, t, :, :], scalar1=st[("nm", a)][:], scalar2=st[("rs", a)][:],
-                op0=ALU.add, op1=ALU.mult,
-            )
-
         def transposes(a, t):
             u = st[("u", a)]
             pa = pst.tile([P, 512], F32, name="pa", tag="pt")
@@ -250,10 +199,7 @@ def tile_colorresblock_t_kernel(tc, x, conv_weight, conv_bias, norm_weight, norm
                 st[("gr", a)] = gr
             gr = st[("gr", a)]
             ht = st[("ht", a)]
-            nc.vector.tensor_copy(
-                out=gr[:, lo:hi, :].rearrange("p (c i) t -> p c t i", i=4),
-                in_=ht[:, :, lo:hi].rearrange("p t (c i) -> p c t i", i=4),
-            )
+            nc.vector.tensor_copy(out=gr[:, lo:hi, :], in_=ht[:, :, lo:hi].rearrange("p t c -> p c t"))
 
         def quantise(a, lo, hi):
             if lo == 0:
@@ -329,36 +275,78 @@ def tile_colorresblock_t_kernel(tc, x, conv_weight, conv_bias, norm_weight, norm
                 hcols = slice((oc - 1) * C * P, (oc + 1) * C * P)
                 nc.sync.dma_start(out=outr[a * P : (a + 1) * P, hcols], in_=ot[:, hcols])
 
+        def mx_pass(a, dst, d, m, ocs):
+            hc = st[("hc", a)]
+            hsc = st[("hsc", a)]
+            nc.tensor.matmul_mx(
+                out=dst,
+                lhsT=hc[:, d * P : (d + 1) * P].bitcast(FP8X4),
+                lhsT_scale=hsc[:, d * P : (d + 1) * P],
+                rhs=wcodes[m][:, ocs].bitcast(FP8X4),
+                rhs_scale=wscales[m][:, ocs],
+                start=True,
+                stop=True,
+            )
+
+        def mx(a, oc):
+            ocs = slice(oc * P, (oc + 1) * P)
+            for e in range(2):
+                pm = psm.tile([P, 512], F32, name="pm")
+                if e == 0:
+                    mx_pass(a, pm[:, 3 * P : 4 * P], C, 1, ocs)
+                for j in range(3):
+                    mx_pass(a, pm[:, j * P : (j + 1) * P], 2 * j + e, 0, ocs)
+                st[("pm", a, oc, e)] = pm
+
+        def second_term(a, oc):
+            cc = work.tile([P, P], F32, name="cc")
+            nc.vector.tensor_tensor(
+                out=cc[:], in0=st[("pm", a, oc, 0)][:, 3 * P : 4 * P], in1=cb[:, oc * P : (oc + 1) * P], op=ALU.add
+            )
+            st[("cc", a, oc)] = cc
+
+        def e1(a, oc):
+            if oc == 0:
+                tt = work.tile([P, 2, 3 * K], F32, name="tt")
+                st[("tt", a)] = tt
+            tt = st[("tt", a)]
+            for e in range(2):
+                pm = st[("pm", a, oc, e)]
+                nc.vector.tensor_tensor(
+                    out=tt[:, e, oc * 3 * P : (oc + 1) * 3 * P].rearrange("p (o j) -> p o j", j=3),
+                    in0=pm[:, 0 : 3 * P].rearrange("p (j o) -> p o j", j=3),
+                    in1=st[("cc", a, oc)][:].unsqueeze(2).to_broadcast([P, P, 3]),
+                    op=ALU.add,
+                )
+
         def piece(g, lag):
             a, r = divmod(g - lag, 4)
             return (a, r) if 0 <= a < NT else None
 
         for g in range(LAG_STATS, 4 * (NT - 1) + LAG_E2 + 4):
-            for i in (2, 4):
-                w = piece(g - i, LAG_STATS)
-                if w and w[1] == 0:
-                    stats_small(w[0], i)
-            w = piece(g, LAG_E1)
+            w = piece(g, LAG_STATS)
             if w:
-                e1(w[0], w[1])
+                stats_piece(w[0], w[1])
+            w1 = piece(g, LAG_E1)
+            if w1:
+                second_term(w1[0], w1[1])
             w = piece(g, 0)
             if w:
                 transposes(w[0], w[1])
                 affine(w[0], w[1])
-            w = piece(g, LAG_STATS)
-            if w:
-                stats_piece(w[0], w[1])
+            w2 = piece(g, LAG_E2)
+            if w2:
+                e2(w2[0], w2[1])
+                if w2[1] == 3 and w2[0] + XBUFS < NT:
+                    load(w2[0] + XBUFS)
+            if w1:
+                e1(w1[0], w1[1])
             w = piece(g, LAG_REGROUP)
             if w and w[1] == 0:
                 regroup(w[0], 0, 512)
             if w and w[1] == 1:
                 quantise(w[0], 0, 512)
                 regroup(w[0], 512, 896)
-            w2 = piece(g, LAG_E2)
-            if w2:
-                e2(w2[0], w2[1])
-                if w2[1] == 3 and w2[0] + XBUFS < NT:
-                    load(w2[0] + XBUFS)
             if w and w[1] == 2:
                 quantise(w[0], 512, 768)
                 quantise(w[0], 768, 896)

@@ -60,32 +60,40 @@ def tile_colorresblock_t_kernel(tc, x, conv_weight, conv_bias, norm_weight, norm
         make_identity(nc, ident[:])
         negh = const.tile([P, 1], F32, name="negh")
         nc.vector.memset(negh[:], -0.5)
+        halfeps = const.tile([P, 1], F32, name="halfeps")
+        nc.vector.memset(halfeps[:], EPS / 2.0)
         junk = const.tile([P, HALF], BF16, name="junk")
+        junk2 = const.tile([P, 2], F32, name="junk2")
+        gbrows = const.tile([P, P], BF16, name="gbrows")
+        nc.vector.memset(gbrows[:], 0.0)
 
         wraw = const.tile([P, 4, 2 * K], BF16, name="wraw")
         nc.sync.dma_start(out=wraw[:], in_=conv_weight.rearrange("(c p) k s -> p c (k s)", p=P))
-        graw = const.tile([P, T], BF16, name="graw")
-        nc.sync.dma_start(out=graw[:], in_=norm_weight.rearrange("(p t) -> p t", t=T))
-        braw = const.tile([P, T], BF16, name="braw")
-        nc.sync.dma_start(out=braw[:], in_=norm_bias.rearrange("(p t) -> p t", t=T))
+        nc.sync.dma_start(out=gbrows[0:T, :], in_=norm_weight.rearrange("(t p) -> t p", p=P))
+        nc.sync.dma_start(out=gbrows[T : 2 * T, :], in_=norm_bias.rearrange("(t p) -> t p", p=P))
         load(1)
         cbraw = const.tile([P, K], BF16, name="cbraw")
         nc.sync.dma_start(out=cbraw[:], in_=conv_bias.partition_broadcast(P))
         for a in range(2, XBUFS):
             load(a)
 
+        gbf = const.tile([P, P], F32, name="gbf")
+        nc.vector.tensor_copy(out=gbf[:], in_=gbrows[:])
+        pg = pst.tile([P, 512], F32, name="pg", tag="pt")
+        nc.tensor.transpose(pg[:, 0:P], gbf[:], ident[:])
         gcol = const.tile([P, T], F32, name="gcol")
-        nc.vector.tensor_copy(out=gcol[:], in_=graw[:])
+        nc.vector.tensor_copy(out=gcol[:], in_=pg[:, 0:T])
         bcol = const.tile([P, T], F32, name="bcol")
-        nc.vector.tensor_copy(out=bcol[:], in_=braw[:])
+        nc.vector.tensor_copy(out=bcol[:], in_=pg[:, T : 2 * T])
         b6col = const.tile([P, T], F32, name="b6col")
-        nc.vector.tensor_scalar(out=b6col[:], in0=braw[:], scalar1=float(C), scalar2=None, op0=ALU.mult)
+        nc.vector.tensor_scalar(out=b6col[:], in0=pg[:, T : 2 * T], scalar1=float(C), scalar2=None, op0=ALU.mult)
 
-        wv = wraw[:].rearrange("p c (q t s) -> p c t q s", t=T, s=2)
-        wf_a = const.tile([P, 4, T, P], F32, name="wf_a")
-        nc.vector.tensor_tensor(out=wf_a[:], in0=wv[:, :, :, :, 0], in1=wv[:, :, :, :, 1], op=ALU.subtract)
-        wf_b = const.tile([P, 4, T, P], F32, name="wf_b")
-        nc.vector.tensor_copy(out=wf_b[:], in_=wv[:, :, :, :, 1])
+        wv = wraw[:].rearrange("p c (k s) -> p c k s", s=2)
+        wf_a = const.tile([P, 4, K], F32, name="wf_a")
+        nc.vector.tensor_tensor(out=wf_a[:], in0=wv[:, :, :, 0], in1=wv[:, :, :, 1], op=ALU.subtract)
+        wf_b = const.tile([P, 4, K], F32, name="wf_b")
+        nc.vector.tensor_copy(out=wf_b[:], in_=wv[:, :, :, 1])
+
         wcodes = []
         wscales = []
         for m, wf in enumerate((wf_a, wf_b)):
@@ -93,7 +101,7 @@ def tile_colorresblock_t_kernel(tc, x, conv_weight, conv_bias, norm_weight, norm
             for oc in range(4):
                 pw = pst.tile([P, 512], F32, name="pw", tag="pt")
                 for t in range(T):
-                    nc.tensor.transpose(pw[:, t * P : (t + 1) * P], wf[:, oc, t, :], ident[:])
+                    nc.tensor.transpose(pw[:, t * P : (t + 1) * P], wf[:, oc, t * P : (t + 1) * P], ident[:])
                 nc.vector.tensor_copy(
                     out=wg[:, oc * P : (oc + 1) * P, :], in_=pw[:].rearrange("p (t o) -> p o t", t=T)
                 )
@@ -122,29 +130,27 @@ def tile_colorresblock_t_kernel(tc, x, conv_weight, conv_bias, norm_weight, norm
                 sq = small.tile([P, 2], F32, name="sq")
                 st[("sq", a)] = sq
             if i < 2:
-                sx = st[("sx", a)]
-                nc.scalar.activation(out=junk[:], in_=xt[:, cols], func=ACT.Identity, accum_out=sx[:, h : h + 1])
+                nc.scalar.activation(
+                    out=junk[:], in_=xt[:, cols], func=ACT.Identity, accum_out=st[("sx", a)][:, h : h + 1]
+                )
             else:
-                sq = st[("sq", a)]
                 nc.scalar.activation(
                     out=junk[:], in_=xt[:, cols], func=ACT.Square, bias=st[("nm", a)][:], scale=1.0,
-                    accum_out=sq[:, h : h + 1],
+                    accum_out=st[("sq", a)][:, h : h + 1],
                 )
-            if i == 1:
+
+        def stats_small(a, i):
+            if i == 2:
                 negmean = small.tile([P, 1], F32, name="negmean")
-                nc.gpsimd.tensor_scalar(
-                    out=negmean[:], in0=sx[:, 0:1], scalar1=sx[:, 1:2], scalar2=-1.0 / ROW,
-                    op0=ALU.add, op1=ALU.mult,
+                nc.scalar.activation(
+                    out=junk2[:], in_=st[("sx", a)][:], func=ACT.Identity, scale=-1.0 / ROW, accum_out=negmean[:]
                 )
                 st[("nm", a)] = negmean
-            if i == 3:
-                var = small.tile([P, 1], F32, name="var")
-                nc.gpsimd.tensor_scalar(
-                    out=var[:], in0=sq[:, 0:1], scalar1=sq[:, 1:2], scalar2=1.0 / ROW, op0=ALU.add, op1=ALU.mult
-                )
+            if i == 4:
                 vare = small.tile([P, 1], F32, name="vare")
-                nc.gpsimd.tensor_scalar(
-                    out=vare[:], in0=var[:], scalar1=1.0, scalar2=EPS, op0=ALU.mult, op1=ALU.add
+                nc.scalar.activation(
+                    out=junk2[:], in_=st[("sq", a)][:], func=ACT.Identity, scale=1.0 / ROW, bias=halfeps[:],
+                    accum_out=vare[:],
                 )
                 rstd = small.tile([P, 1], F32, name="rstd")
                 nc.gpsimd.tensor_tensor(out=rstd[:], in0=vare[:], in1=negh[:], op=ALU.pow)
@@ -155,11 +161,16 @@ def tile_colorresblock_t_kernel(tc, x, conv_weight, conv_bias, norm_weight, norm
                 u = work.tile([P, T, C, P], F32, name="u")
                 st[("u", a)] = u
             u = st[("u", a)]
-            xv = st[("x", a)][:].rearrange("p (q t d) -> p t d q", t=T, d=C)
-            nc.vector.tensor_scalar(
-                out=u[:, t, :, :], in0=xv[:, t, :, :], scalar1=st[("nm", a)][:], scalar2=st[("rs", a)][:],
-                op0=ALU.add, op1=ALU.mult,
-            )
+            xv = st[("x", a)][:].rearrange("p (t q d) -> p t q d", t=T, d=C)
+            for lo in (0, 3):
+                nc.vector.tensor_scalar(
+                    out=u[:, t, lo : lo + 3, :].rearrange("p d q -> p q d"),
+                    in0=xv[:, t, :, lo : lo + 3],
+                    scalar1=st[("nm", a)][:],
+                    scalar2=st[("rs", a)][:],
+                    op0=ALU.add,
+                    op1=ALU.mult,
+                )
 
         def transposes(a, t):
             u = st[("u", a)]
@@ -199,7 +210,10 @@ def tile_colorresblock_t_kernel(tc, x, conv_weight, conv_bias, norm_weight, norm
                 st[("gr", a)] = gr
             gr = st[("gr", a)]
             ht = st[("ht", a)]
-            nc.vector.tensor_copy(out=gr[:, lo:hi, :], in_=ht[:, :, lo:hi].rearrange("p t c -> p c t"))
+            nc.vector.tensor_copy(
+                out=gr[:, lo:hi, :].rearrange("p (c i) t -> p c t i", i=4),
+                in_=ht[:, :, lo:hi].rearrange("p t (c i) -> p c t i", i=4),
+            )
 
         def quantise(a, lo, hi):
             if lo == 0:
@@ -275,78 +289,36 @@ def tile_colorresblock_t_kernel(tc, x, conv_weight, conv_bias, norm_weight, norm
                 hcols = slice((oc - 1) * C * P, (oc + 1) * C * P)
                 nc.sync.dma_start(out=outr[a * P : (a + 1) * P, hcols], in_=ot[:, hcols])
 
-        def mx_pass(a, dst, d, m, ocs):
-            hc = st[("hc", a)]
-            hsc = st[("hsc", a)]
-            nc.tensor.matmul_mx(
-                out=dst,
-                lhsT=hc[:, d * P : (d + 1) * P].bitcast(FP8X4),
-                lhsT_scale=hsc[:, d * P : (d + 1) * P],
-                rhs=wcodes[m][:, ocs].bitcast(FP8X4),
-                rhs_scale=wscales[m][:, ocs],
-                start=True,
-                stop=True,
-            )
-
-        def mx(a, oc):
-            ocs = slice(oc * P, (oc + 1) * P)
-            for e in range(2):
-                pm = psm.tile([P, 512], F32, name="pm")
-                if e == 0:
-                    mx_pass(a, pm[:, 3 * P : 4 * P], C, 1, ocs)
-                for j in range(3):
-                    mx_pass(a, pm[:, j * P : (j + 1) * P], 2 * j + e, 0, ocs)
-                st[("pm", a, oc, e)] = pm
-
-        def second_term(a, oc):
-            cc = work.tile([P, P], F32, name="cc")
-            nc.vector.tensor_tensor(
-                out=cc[:], in0=st[("pm", a, oc, 0)][:, 3 * P : 4 * P], in1=cb[:, oc * P : (oc + 1) * P], op=ALU.add
-            )
-            st[("cc", a, oc)] = cc
-
-        def e1(a, oc):
-            if oc == 0:
-                tt = work.tile([P, 2, 3 * K], F32, name="tt")
-                st[("tt", a)] = tt
-            tt = st[("tt", a)]
-            for e in range(2):
-                pm = st[("pm", a, oc, e)]
-                nc.vector.tensor_tensor(
-                    out=tt[:, e, oc * 3 * P : (oc + 1) * 3 * P].rearrange("p (o j) -> p o j", j=3),
-                    in0=pm[:, 0 : 3 * P].rearrange("p (j o) -> p o j", j=3),
-                    in1=st[("cc", a, oc)][:].unsqueeze(2).to_broadcast([P, P, 3]),
-                    op=ALU.add,
-                )
-
         def piece(g, lag):
             a, r = divmod(g - lag, 4)
             return (a, r) if 0 <= a < NT else None
 
         for g in range(LAG_STATS, 4 * (NT - 1) + LAG_E2 + 4):
-            w = piece(g, LAG_STATS)
+            for i in (2, 4):
+                w = piece(g - i, LAG_STATS)
+                if w and w[1] == 0:
+                    stats_small(w[0], i)
+            w = piece(g, LAG_E1)
             if w:
-                stats_piece(w[0], w[1])
-            w1 = piece(g, LAG_E1)
-            if w1:
-                second_term(w1[0], w1[1])
+                e1(w[0], w[1])
             w = piece(g, 0)
             if w:
                 transposes(w[0], w[1])
                 affine(w[0], w[1])
-            w2 = piece(g, LAG_E2)
-            if w2:
-                e2(w2[0], w2[1])
-                if w2[1] == 3 and w2[0] + XBUFS < NT:
-                    load(w2[0] + XBUFS)
-            if w1:
-                e1(w1[0], w1[1])
+            w = piece(g, LAG_STATS)
+            if w:
+                stats_piece(w[0], w[1])
             w = piece(g, LAG_REGROUP)
             if w and w[1] == 0:
                 regroup(w[0], 0, 512)
             if w and w[1] == 1:
                 quantise(w[0], 0, 512)
                 regroup(w[0], 512, 896)
+            w2 = piece(g, LAG_E2)
+            if w2:
+                e2(w2[0], w2[1])
+                if w2[1] == 3 and w2[0] + XBUFS < NT:
+                    load(w2[0] + XBUFS)
             if w and w[1] == 2:
                 quantise(w[0], 512, 768)
                 quantise(w[0], 768, 896)

@@ -162,10 +162,12 @@ def tile_colorresblock_t_kernel(tc, x, conv_weight, conv_bias, norm_weight, norm
                 st[("u", a)] = u
             u = st[("u", a)]
             xv = st[("x", a)][:].rearrange("p (t q d) -> p t q d", t=T, d=C)
+            if t % 2 == 1:
+                return
             for lo in (0, 3):
                 nc.vector.tensor_scalar(
-                    out=u[:, t, lo : lo + 3, :].rearrange("p d q -> p q d"),
-                    in0=xv[:, t, :, lo : lo + 3],
+                    out=u[:, t : t + 2, lo : lo + 3, :].rearrange("p t d q -> p t q d"),
+                    in0=xv[:, t : t + 2, :, lo : lo + 3],
                     scalar1=st[("nm", a)][:],
                     scalar2=st[("rs", a)][:],
                     op0=ALU.add,
@@ -273,13 +275,15 @@ def tile_colorresblock_t_kernel(tc, x, conv_weight, conv_bias, norm_weight, norm
             if oc == 0:
                 ot = work.tile([P, ROW], F32, name="ot")
                 st[("ot", a)] = ot
+            if oc % 2 == 0:
+                return
             ot = st[("ot", a)]
             tt = st[("tt", a)]
             xt = st[("x", a)]
-            cols = slice(oc * C * P, (oc + 1) * C * P)
+            cols = slice((oc - 1) * C * P, (oc + 1) * C * P)
             nc.vector.scalar_tensor_tensor(
                 out=ot[:, cols].rearrange("p (a e) -> p a e", e=2),
-                in0=tt[:, :, oc * 3 * P : (oc + 1) * 3 * P].rearrange("p e a -> p a e"),
+                in0=tt[:, :, (oc - 1) * 3 * P : (oc + 1) * 3 * P].rearrange("p e a -> p a e"),
                 scalar=0.0,
                 in1=xt[:, cols].rearrange("p (a e) -> p a e", e=2),
                 op0=ALU.max,

from contextlib import ExitStack

import concourse.mybir as mybir
from concourse.masks import make_identity

F32 = mybir.dt.float32
BF16 = mybir.dt.bfloat16
U32 = mybir.dt.uint32
U8 = mybir.dt.uint8
FP8X4 = mybir.dt.float8_e4m3fn_x4
ALU = mybir.AluOpType
ACT = mybir.ActivationFunctionType

P = 128
K = 512
C = 6
T = 4
ROW = K * C
HALF = ROW // 2
NPOS = 80 * 24
NT = NPOS // P
EPS = 1e-5
HCOLS = (C + 1) * P
XBUFS = 7

FLOPS = 2 * NPOS * C * K * K + 2 * NPOS * K * K

LAG_STATS = -8
LAG_NORM = -2
LAG_REGROUP = 4
LAG_MX = 7
LAG_E1 = 8
LAG_E2 = 9


def tile_colorresblock_t_kernel(tc, x, conv_weight, conv_bias, norm_weight, norm_bias, out):
    nc = tc.nc
    xr = x.flatten_outer_dims()
    outr = out.flatten_outer_dims()

    with ExitStack() as ctx:
        const = ctx.enter_context(tc.tile_pool(name="const", bufs=1))
        xpool = ctx.enter_context(tc.tile_pool(name="xpool", bufs=XBUFS))
        small = ctx.enter_context(tc.tile_pool(name="small", bufs=4))
        work = ctx.enter_context(tc.tile_pool(name="work", bufs=2))
        pst = ctx.enter_context(tc.psum_pool(name="pst", bufs=4))
        psm = ctx.enter_context(tc.psum_pool(name="psm", bufs=4))
        ctx.enter_context(tc.manual_schedule())

        st = {}

        def load(a):
            xt = xpool.tile([P, ROW], BF16, name="xt")
            nc.sync.dma_start(out=xt[:], in_=xr[a * P : (a + 1) * P, :])
            st[("x", a)] = xt

        load(0)

        ident = const.tile([P, P], F32, name="ident")
        make_identity(nc, ident[:])
        negh = const.tile([P, 1], F32, name="negh")
        nc.vector.memset(negh[:], -0.5)
        halfeps = const.tile([P, 1], F32, name="halfeps")
        nc.vector.memset(halfeps[:], EPS / 2.0)
        junk = const.tile([P, HALF], BF16, name="junk")
        junk2 = const.tile([P, 2], F32, name="junk2")
        gbrows = const.tile([P, P], BF16, name="gbrows")
        nc.vector.memset(gbrows[:], 0.0)

        wraw = const.tile([P, 4, 2 * K], BF16, name="wraw")
        nc.sync.dma_start(out=wraw[:], in_=conv_weight.rearrange("(c p) k s -> p c (k s)", p=P))
        nc.sync.dma_start(out=gbrows[0:T, :], in_=norm_weight.rearrange("(t p) -> t p", p=P))
        nc.sync.dma_start(out=gbrows[T : 2 * T, :], in_=norm_bias.rearrange("(t p) -> t p", p=P))
        load(1)
        cbraw = const.tile([P, K], BF16, name="cbraw")
        nc.sync.dma_start(out=cbraw[:], in_=conv_bias.partition_broadcast(P))
        for a in range(2, XBUFS):
            load(a)

        gbf = const.tile([P, P], F32, name="gbf")
        nc.vector.tensor_copy(out=gbf[:], in_=gbrows[:])
        pg = pst.tile([P, 512], F32, name="pg", tag="pt")
        nc.tensor.transpose(pg[:, 0:P], gbf[:], ident[:])
        gcol = const.tile([P, T], F32, name="gcol")
        nc.vector.tensor_copy(out=gcol[:], in_=pg[:, 0:T])
        bcol = const.tile([P, T], F32, name="bcol")
        nc.vector.tensor_copy(out=bcol[:], in_=pg[:, T : 2 * T])
        b6col = const.tile([P, T], F32, name="b6col")
        nc.vector.tensor_scalar(out=b6col[:], in0=pg[:, T : 2 * T], scalar1=float(C), scalar2=None, op0=ALU.mult)

        wv = wraw[:].rearrange("p c (k s) -> p c k s", s=2)
        wf_a = const.tile([P, 4, K], F32, name="wf_a")
        nc.vector.tensor_tensor(out=wf_a[:], in0=wv[:, :, :, 0], in1=wv[:, :, :, 1], op=ALU.subtract)
        wf_b = const.tile([P, 4, K], F32, name="wf_b")
        nc.vector.tensor_copy(out=wf_b[:], in_=wv[:, :, :, 1])

        wcodes = []
        wscales = []
        for m, wf in enumerate((wf_a, wf_b)):
            wg = const.tile([P, K, T], BF16, name="wg%d" % m, align_bytes=64)
            for oc in range(4):
                pw = pst.tile([P, 512], F32, name="pw", tag="pt")
                for t in range(T):
                    nc.tensor.transpose(pw[:, t * P : (t + 1) * P], wf[:, oc, t * P : (t + 1) * P], ident[:])
                nc.vector.tensor_copy(
                    out=wg[:, oc * P : (oc + 1) * P, :], in_=pw[:].rearrange("p (t o) -> p o t", t=T)
                )
            wc = const.tile([P, K], U32, name="wc%d" % m, align_bytes=64)
            ws = const.tile([P, K], U8, name="ws%d" % m, align_bytes=64)
            wcodes.append(wc)
            wscales.append(ws)
            st[("wg", m)] = wg
        for m in range(2):
            nc.vector.quantize_mx(
                out=wcodes[m][:].bitcast(FP8X4),
                scales=wscales[m][:],
                in_=st[("wg", m)][:].rearrange("p o t -> p (o t)"),
            )
        cb = const.tile([P, K], F32, name="cb")
        nc.vector.tensor_copy(out=cb[:], in_=cbraw[:])

        def stats_piece(a, i):
            xt = st[("x", a)]
            h = i % 2
            cols = slice(h * HALF, (h + 1) * HALF)
            if i == 0:
                sx = small.tile([P, 2], F32, name="sx")
                st[("sx", a)] = sx
            if i == 2:
                sq = small.tile([P, 2], F32, name="sq")
                st[("sq", a)] = sq
            if i < 2:
                nc.scalar.activation(
                    out=junk[:], in_=xt[:, cols], func=ACT.Identity, accum_out=st[("sx", a)][:, h : h + 1]
                )
            else:
                nc.scalar.activation(
                    out=junk[:], in_=xt[:, cols], func=ACT.Square, bias=st[("nm", a)][:], scale=1.0,
                    accum_out=st[("sq", a)][:, h : h + 1],
                )

        def stats_small(a, i):
            if i == 2:
                negmean = small.tile([P, 1], F32, name="negmean")
                nc.scalar.activation(
                    out=junk2[:], in_=st[("sx", a)][:], func=ACT.Identity, scale=-1.0 / ROW, accum_out=negmean[:]
                )
                st[("nm", a)] = negmean
            if i == 4:
                vare = small.tile([P, 1], F32, name="vare")
                nc.scalar.activation(
                    out=junk2[:], in_=st[("sq", a)][:], func=ACT.Identity, scale=1.0 / ROW, bias=halfeps[:],
                    accum_out=vare[:],
                )
                rstd = small.tile([P, 1], F32, name="rstd")
                nc.gpsimd.tensor_tensor(out=rstd[:], in0=vare[:], in1=negh[:], op=ALU.pow)
                st[("rs", a)] = rstd

        def norm_piece(a, t):
            if t == 0:
                u = work.tile([P, T, C, P], F32, name="u")
                st[("u", a)] = u
            u = st[("u", a)]
            xv = st[("x", a)][:].rearrange("p (t q d) -> p t q d", t=T, d=C)
            if t % 2 == 1:
                return
            for lo in (0, 3):
                nc.vector.tensor_scalar(
                    out=u[:, t : t + 2, lo : lo + 3, :].rearrange("p t d q -> p t q d"),
                    in0=xv[:, t : t + 2, :, lo : lo + 3],
                    scalar1=st[("nm", a)][:],
                    scalar2=st[("rs", a)][:],
                    op0=ALU.add,
                    op1=ALU.mult,
                )

        def transposes(a, t):
            u = st[("u", a)]
            pa = pst.tile([P, 512], F32, name="pa", tag="pt")
            for d in range(4):
                nc.tensor.transpose(pa[:, d * P : (d + 1) * P], u[:, t, d, :], ident[:])
            pb = pst.tile([P, 512], F32, name="pb", tag="pt")
            for d in range(4, C):
                nc.tensor.transpose(pb[:, (d - 4) * P : (d - 3) * P], u[:, t, d, :], ident[:])
            for d in range(C):
                nc.tensor.matmul(
                    pb[:, 2 * P : 3 * P], lhsT=u[:, t, d, :], rhs=ident[:], is_transpose=True,
                    start=(d == 0), stop=(d == C - 1),
                )
            st[("pa", a, t)] = pa
            st[("pb", a, t)] = pb

        def affine(a, t):
            if t == 0:
                ht = work.tile([P, T, HCOLS], BF16, name="ht")
                st[("ht", a)] = ht
            ht = st[("ht", a)]
            pa = st[("pa", a, t)]
            pb = st[("pb", a, t)]
            g = gcol[:, t : t + 1]
            b = bcol[:, t : t + 1]
            nc.scalar.activation(out=ht[:, t, 0 : 4 * P], in_=pa[:], func=ACT.Identity, scale=g, bias=b)
            nc.scalar.activation(out=ht[:, t, 4 * P : 6 * P], in_=pb[:, 0 : 2 * P], func=ACT.Identity, scale=g, bias=b)
            nc.scalar.activation(
                out=ht[:, t, 6 * P : 7 * P], in_=pb[:, 2 * P : 3 * P], func=ACT.Identity, scale=g,
                bias=b6col[:, t : t + 1],
            )

        def regroup(a, lo, hi):
            if lo == 0:
                gr = work.tile([P, HCOLS, T], BF16, name="gr", align_bytes=64)
                st[("gr", a)] = gr
            gr = st[("gr", a)]
            ht = st[("ht", a)]
            nc.vector.tensor_copy(
                out=gr[:, lo:hi, :].rearrange("p (c i) t -> p c t i", i=4),
                in_=ht[:, :, lo:hi].rearrange("p t (c i) -> p c t i", i=4),
            )

        def quantise(a, lo, hi):
            if lo == 0:
                hc = work.tile([P, HCOLS], U32, name="hc", align_bytes=64)
                hsc = work.tile([P, HCOLS], U8, name="hsc", align_bytes=64)
                st[("hc", a)] = hc
                st[("hsc", a)] = hsc
            nc.vector.quantize_mx(
                out=st[("hc", a)][:, lo:hi].bitcast(FP8X4),
                scales=st[("hsc", a)][:, lo:hi],
                in_=st[("gr", a)][:, lo:hi, :].rearrange("p c t -> p (c t)"),
            )

        def mx(a, oc):
            hc = st[("hc", a)]
            hsc = st[("hsc", a)]
            ocs = slice(oc * P, (oc + 1) * P)
            for e in range(2):
                pm = psm.tile([P, 512], F32, name="pm")
                for j in range(3):
                    d = 2 * j + e
                    nc.tensor.matmul_mx(
                        out=pm[:, j * P : (j + 1) * P],
                        lhsT=hc[:, d * P : (d + 1) * P].bitcast(FP8X4),
                        lhsT_scale=hsc[:, d * P : (d + 1) * P],
                        rhs=wcodes[0][:, ocs].bitcast(FP8X4),
                        rhs_scale=wscales[0][:, ocs],
                        start=True,
                        stop=False,
                    )
                    nc.tensor.matmul_mx(
                        out=pm[:, j * P : (j + 1) * P],
                        lhsT=hc[:, C * P : (C + 1) * P].bitcast(FP8X4),
                        lhsT_scale=hsc[:, C * P : (C + 1) * P],
                        rhs=wcodes[1][:, ocs].bitcast(FP8X4),
                        rhs_scale=wscales[1][:, ocs],
                        start=False,
                        stop=True,
                    )
                st[("pm", a, oc, e)] = pm

        def e1(a, oc):
            if oc == 0:
                tt = work.tile([P, 2, 3 * K], F32, name="tt")
                st[("tt", a)] = tt
            tt = st[("tt", a)]
            for e in range(2):
                pm = st[("pm", a, oc, e)]
                nc.vector.tensor_tensor(
                    out=tt[:, e, oc * 3 * P : (oc + 1) * 3 * P].rearrange("p (o j) -> p o j", j=3),
                    in0=pm[:, 0 : 3 * P].rearrange("p (j o) -> p o j", j=3),
                    in1=cb[:, oc * P : (oc + 1) * P].unsqueeze(2).to_broadcast([P, P, 3]),
                    op=ALU.add,
                )

        def e2(a, oc):
            if oc == 0:
                ot = work.tile([P, ROW], F32, name="ot")
                st[("ot", a)] = ot
            if oc % 2 == 0:
                return
            ot = st[("ot", a)]
            tt = st[("tt", a)]
            xt = st[("x", a)]
            cols = slice((oc - 1) * C * P, (oc + 1) * C * P)
            nc.vector.scalar_tensor_tensor(
                out=ot[:, cols].rearrange("p (a e) -> p a e", e=2),
                in0=tt[:, :, (oc - 1) * 3 * P : (oc + 1) * 3 * P].rearrange("p e a -> p a e"),
                scalar=0.0,
                in1=xt[:, cols].rearrange("p (a e) -> p a e", e=2),
                op0=ALU.max,
                op1=ALU.add,
            )
            if oc % 2 == 1:
                hcols = slice((oc - 1) * C * P, (oc + 1) * C * P)
                nc.sync.dma_start(out=outr[a * P : (a + 1) * P, hcols], in_=ot[:, hcols])

        def piece(g, lag):
            a, r = divmod(g - lag, 4)
            return (a, r) if 0 <= a < NT else None

        for g in range(LAG_STATS, 4 * (NT - 1) + LAG_E2 + 4):
            for i in (2, 4):
                w = piece(g - i, LAG_STATS)
                if w and w[1] == 0:
                    stats_small(w[0], i)
            w = piece(g, LAG_E1)
            if w:
                e1(w[0], w[1])
            w = piece(g, 0)
            if w:
                transposes(w[0], w[1])
                affine(w[0], w[1])
            w = piece(g, LAG_STATS)
            if w:
                stats_piece(w[0], w[1])
            w = piece(g, LAG_REGROUP)
            if w and w[1] == 0:
                regroup(w[0], 0, 512)
            if w and w[1] == 1:
                quantise(w[0], 0, 512)
                regroup(w[0], 512, 896)
            w2 = piece(g, LAG_E2)
            if w2:
                e2(w2[0], w2[1])
                if w2[1] == 3 and w2[0] + XBUFS < NT:
                    load(w2[0] + XBUFS)
            if w and w[1] == 2:
                quantise(w[0], 512, 768)
                quantise(w[0], 768, 896)
            w = piece(g, LAG_NORM)
            if w:
                norm_piece(w[0], w[1])
            w = piece(g, LAG_MX)
            if w:
                mx(w[0], w[1])
